import numpy as np
import ml_dtypes


def mxq(x, axis, fmt="e4m3"):
    dtype, down = {"e4m3": (ml_dtypes.float8_e4m3fn, 7), "e5m2": (ml_dtypes.float8_e5m2, 14)}[fmt]
    v = np.moveaxis(np.asarray(x, np.float32).astype(ml_dtypes.bfloat16).astype(np.float64), axis, -1)
    blocks = v.reshape(v.shape[:-1] + (-1, 32))
    amax = np.abs(blocks).max(-1, keepdims=True)
    byte = np.maximum(np.where(amax > 0, np.frexp(amax)[1] - 1 + 127, 0) - down, 1)
    scale = np.exp2(byte - 127.0)
    codes = (blocks / scale).astype(np.float32).astype(dtype).astype(np.float64)
    return np.moveaxis((codes * scale).reshape(v.shape), -1, axis)


WIDE = False


def mx_kscale(k):
    if not WIDE:
        return np.ones(k)
    levels = np.array([10, -10, 5, -5, 0])
    a = np.random.permutation(np.resize(levels, k // 512 * 4)).reshape(k // 512, 4)
    idx = np.arange(k)
    return np.exp2(a[idx // 512, idx % 128 // 32])


BF16 = ml_dtypes.bfloat16


def bf(x):
    return np.asarray(x, np.float32).astype(BF16)


def f64(x):
    return np.asarray(x).astype(np.float64)


B, C, D, H, ST = 32, 32, 1024, 16, 4
HD = D // H
HP = HD // 2
CS = C // ST
EPS = 1.1920929e-07


def rmsnorm(x, w):
    ms = np.mean(np.square(x), axis=-1, keepdims=True)
    return x * (1.0 / np.sqrt(ms + EPS)) * w


def rope_freqs(t):
    end = 2595.0 * np.log10(1.0 + 4000.0 / 200.0)
    scale = np.power(10.0, np.linspace(0.0, end, HP) / 2595.0) - 1.0
    base = 200.0 * scale / 1000.0
    return t[:, None] * base[None, :]


def rope(x, freqs):
    xr = x.reshape(*x.shape[:-1], HP, 2)
    a, b = xr[..., 0], xr[..., 1]
    cos, sin = np.cos(freqs), np.sin(freqs)
    return np.stack([a * cos - b * sin, a * sin + b * cos], axis=-1).reshape(x.shape)


def setup_inputs():
    s = mx_kscale(D)
    tok = np.exp2(np.random.uniform(-1.5, 1.5, (B, C, 1)))
    return {"x": bf(np.random.standard_normal((B, C, D)) * tok),
            "rmskv_w": bf((1.0 + 0.1 * np.random.standard_normal(D)) * s),
            "kv_w": bf(np.random.standard_normal((D, 2 * D)) / np.sqrt(D) / s[:, None]),
            "kv_b": bf(np.random.standard_normal(2 * D) * 0.3),
            "ln_w": bf(1.0 + 0.1 * np.random.standard_normal(HD))}


def reference(x, rmskv_w, kv_w, kv_b, ln_w):
    xs = f64(x)[:, ::ST, :]
    xn = rmsnorm(xs, f64(rmskv_w))
    kv = (mxq(xn, 2, "e4m3") @ mxq(f64(kv_w), 0, "e4m3")) + f64(kv_b)
    kv = kv.reshape(B, CS, 2, H, HD)
    k = kv[:, :, 0].transpose(0, 2, 1, 3)
    v = kv[:, :, 1].transpose(0, 2, 1, 3)
    k = rope(k, rope_freqs(np.arange(C, dtype=np.float64)[::ST]))
    return rmsnorm(k, f64(ln_w)), v

@@ -1,0 +1,301 @@
+import concourse.mybir as mybir
+from concourse.masks import make_identity
+
+F32 = mybir.dt.float32
+BF16 = mybir.dt.bfloat16
+I32 = mybir.dt.int32
+U32 = mybir.dt.uint32
+U8 = mybir.dt.uint8
+FP8X4 = mybir.dt.float8_e4m3fn_x4
+ALU = mybir.AluOpType
+ACT = mybir.ActivationFunctionType
+AXIS = mybir.AxisListType
+
+B, C, D, H, ST = 32, 32, 1024, 16, 4
+HD = D // H
+HP = HD // 2
+CS = C // ST
+EPS = 1.1920929e-07
+
+P = 128
+PACK = 4
+K_PASS = P * PACK
+PASSES = D // K_PASS
+TOKEN_TILES = B * CS // P
+ROWS = P // B
+N_TILE = 512
+CHUNKS = 2 * D // N_TILE
+KEY_CHUNKS = D // N_TILE
+HEADS = N_TILE // HD
+
+PI = 3.141592653589793
+TWO_PI = 2.0 * PI
+TWO_PI_HIGH = 6.28125
+TWO_PI_LOW = TWO_PI - TWO_PI_HIGH
+ROUND_TO_INTEGER = 1.5 * 2.0**23
+
+FLOPS = 2 * B * CS * D * 2 * D
+BYTES = 2 * (B * CS * D + D * 2 * D + D + 2 * D + HD) + 4 * 2 * B * CS * D
+
+
+def angle_steps():
+    top = 1.0 + 4000.0 / 200.0
+    steps = []
+    for j in range(HP):
+        base = 200.0 * (top ** (j / (HP - 1)) - 1.0) / 1000.0
+        step = ST * base
+        steps.append(step - TWO_PI * round(step / TWO_PI))
+    return steps
+
+
+def rotation_tables(nc, keep, ln_w):
+    ln_gain = keep.tile([P, HD], BF16)
+    nc.scalar.dma_start(out=ln_gain[:], in_=ln_w.partition_broadcast(P))
+    gain_halves = ln_gain[:].rearrange("p (j e) -> p e j", e=2)
+
+    partition = keep.tile([P, 1], I32)
+    nc.gpsimd.iota(partition[:], pattern=[[0, 1]], base=0, channel_multiplier=1)
+    row = keep.tile([P, 1], I32)
+    nc.vector.tensor_single_scalar(out=row[:], in_=partition[:], scalar=ROWS - 1, op=ALU.bitwise_and)
+    position = keep.tile([P, TOKEN_TILES], F32)
+    nc.vector.tensor_copy(out=position[:, 0:1], in_=row[:])
+    for i in range(1, TOKEN_TILES):
+        nc.vector.tensor_scalar_add(out=position[:, i : i + 1], in0=position[:, 0:1], scalar1=float(ROWS * i))
+
+    phase = keep.tile([P, 2, TOKEN_TILES, HP], F32)
+    for j, step in enumerate(angle_steps()):
+        nc.vector.tensor_scalar_mul(out=phase[:, 0, :, j], in0=position[:], scalar1=step)
+    nc.vector.tensor_scalar_add(out=phase[:, 1], in0=phase[:, 0], scalar1=0.5 * PI)
+
+    turns = keep.tile([P, 2, TOKEN_TILES, HP], F32)
+    nc.vector.tensor_scalar(
+        out=turns[:], in0=phase[:], scalar1=1.0 / TWO_PI, scalar2=ROUND_TO_INTEGER, op0=ALU.mult, op1=ALU.add
+    )
+    nc.vector.tensor_scalar_sub(out=turns[:], in0=turns[:], scalar1=ROUND_TO_INTEGER)
+    flat = "p a i j -> p (a i j)"
+    nc.vector.scalar_tensor_tensor(
+        out=phase[:].rearrange(flat), in0=turns[:].rearrange(flat), scalar=-TWO_PI_HIGH,
+        in1=phase[:].rearrange(flat), op0=ALU.mult, op1=ALU.add,
+    )
+    nc.vector.scalar_tensor_tensor(
+        out=phase[:].rearrange(flat), in0=turns[:].rearrange(flat), scalar=-TWO_PI_LOW,
+        in1=phase[:].rearrange(flat), op0=ALU.mult, op1=ALU.add,
+    )
+    sin_cos = keep.tile([P, 2, TOKEN_TILES, HP], F32)
+    nc.scalar.activation(out=sin_cos[:], in_=phase[:], func=ACT.Sin)
+    sin, cos = sin_cos[:, 0], sin_cos[:, 1]
+
+    same = keep.tile([P, TOKEN_TILES, 2, HP], F32)
+    cross = keep.tile([P, TOKEN_TILES, 2, HP], F32)
+    shape = [P, TOKEN_TILES, HP]
+    for e in range(2):
+        gain = gain_halves[:, e, :].unsqueeze(1).to_broadcast(shape)
+        nc.vector.tensor_tensor(out=same[:, :, e, :], in0=cos, in1=gain, op=ALU.mult)
+    nc.vector.tensor_tensor(
+        out=cross[:, :, 0, :], in0=sin, in1=gain_halves[:, 1, :].unsqueeze(1).to_broadcast(shape), op=ALU.mult
+    )
+    nc.vector.scalar_tensor_tensor(
+        out=cross[:, :, 1, :], in0=sin, scalar=-1.0,
+        in1=gain_halves[:, 0, :].unsqueeze(1).to_broadcast(shape), op0=ALU.mult, op1=ALU.mult,
+    )
+    return same, cross
+
+
+def inverse_rms(nc, small, minus_half, sum_sq, count, width, name):
+    mean_sq = small.tile([P, width], F32, name="mean_sq_" + name)
+    nc.gpsimd.tensor_scalar(
+        out=mean_sq[:], in0=sum_sq[:], scalar1=1.0 / count, scalar2=EPS, op0=ALU.mult, op1=ALU.add
+    )
+    inverse = small.tile([P, width], F32, name="inverse_" + name)
+    nc.gpsimd.tensor_tensor(out=inverse[:], in0=mean_sq[:], in1=minus_half[:, 0:width], op=ALU.pow)
+    return inverse
+
+
+def tile_attention_pb_kernel(tc, x, rmskv_w, kv_w, kv_b, ln_w, out_0, out_1):
+    nc = tc.nc
+    with (
+        tc.tile_pool(name="keep", bufs=1) as keep,
+        tc.tile_pool(name="stage", bufs=3) as stage,
+        tc.tile_pool(name="small", bufs=4) as small,
+        tc.psum_pool(name="flipped", bufs=4) as flipped,
+        tc.psum_pool(name="products", bufs=4) as products,
+        tc.manual_schedule(),
+    ):
+        x_sb = keep.tile([P, TOKEN_TILES, D], BF16)
+        x_rows = x.rearrange("b (i r s) f -> r s b i f", i=TOKEN_TILES, r=ROWS, s=ST)
+        for r in range(ROWS):
+            nc.sync.dma_start(out=x_sb[r:P:ROWS, :, :], in_=x_rows[r, 0])
+
+        rms_gain = keep.tile([P, PASSES, PACK], BF16)
+        nc.scalar.dma_start(out=rms_gain[:], in_=rmskv_w.rearrange("(g p t) -> p g t", g=PASSES, t=PACK))
+
+        bias = keep.tile([P, 2 * D], BF16)
+        w_rows = kv_w.rearrange("(g p t) n -> g p t n", g=PASSES, t=PACK)
+        w_raw = {}
+        for n in range(CHUNKS):
+            if n == KEY_CHUNKS:
+                nc.sync.dma_start(out=bias[:], in_=kv_b.partition_broadcast(P))
+            for g in range(PASSES):
+                w_raw[n, g] = keep.tile([P, PACK, N_TILE], BF16, name="w_raw_%d_%d" % (n, g))
+                nc.sync.dma_start(out=w_raw[n, g][:], in_=w_rows[g, :, :, n * N_TILE : (n + 1) * N_TILE])
+
+        same, cross = rotation_tables(nc, keep, ln_w)
+        minus_half = keep.tile([P, HEADS], F32)
+        nc.gpsimd.memset(minus_half[:], -0.5)
+        identity = keep.tile([P, P], F32)
+        make_identity(nc, identity[:])
+
+        w_grouped, w_codes, w_scales = {}, {}, {}
+
+        def regroup(engine_copy, n, g):
+            w_grouped[n, g] = stage.tile([P, N_TILE, PACK], BF16, name="w_grouped", align_bytes=64)
+            engine_copy(
+                out=w_grouped[n, g][:].rearrange("p (c i) t -> p c t i", i=4),
+                in_=w_raw[n, g][:].rearrange("p t (c i) -> p c t i", i=4),
+            )
+
+        def quantise(n, g):
+            w_codes[n, g] = keep.tile([P, N_TILE], U32, name="w_codes_%d_%d" % (n, g), align_bytes=64)
+            w_scales[n, g] = keep.tile([P, N_TILE], U8, name="w_scales_%d_%d" % (n, g), align_bytes=64)
+            nc.vector.quantize_mx(
+                out=w_codes[n, g][:].bitcast(FP8X4), scales=w_scales[n, g][:],
+                in_=w_grouped[n, g][:].rearrange("p w t -> p (w t)"),
+            )
+
+        x_inverse, x_turned, x_codes, x_scales = {}, {}, {}, {}
+
+        def token_norm(i):
+            squares = stage.tile([P, D], BF16)
+            sum_sq = small.tile([P, 1], F32)
+            nc.scalar.activation(out=squares[:], in_=x_sb[:, i, :], func=ACT.Square, accum_out=sum_sq[:])
+            x_inverse[i] = inverse_rms(nc, small, minus_half, sum_sq, D, 1, "x")
+
+        def turn_tokens(i):
+            scaled = stage.tile([P, PASSES, PACK, P], F32)
+            nc.scalar.activation(
+                out=scaled[:], in_=x_sb[:, i, :].rearrange("p (g q t) -> p g t q", g=PASSES, t=PACK),
+                func=ACT.Copy, scale=x_inverse[i][:, 0:1],
+            )
+            for g in range(PASSES):
+                x_turned[i, g] = flipped.tile([P, PACK, P], F32, name="turned")
+                for t in range(PACK):
+                    nc.tensor.transpose(x_turned[i, g][:, t, :], scaled[:, g, t, :], identity[:])
+
+        def quantise_tokens(i):
+            grouped = stage.tile([P, PASSES, P, PACK], BF16, name="x_grouped", align_bytes=64)
+            for g in range(PASSES):
+                nc.vector.tensor_tensor(
+                    out=grouped[:, g], in0=x_turned[i, g][:].rearrange("p t r -> p r t"),
+                    in1=rms_gain[:, g, :].unsqueeze(1).to_broadcast([P, P, PACK]), op=ALU.mult,
+                )
+            x_codes[i] = keep.tile([P, PASSES * P], U32, name="x_codes_%d" % i, align_bytes=64)
+            x_scales[i] = keep.tile([P, PASSES * P], U8, name="x_scales_%d" % i, align_bytes=64)
+            nc.vector.quantize_mx(
+                out=x_codes[i][:].bitcast(FP8X4), scales=x_scales[i][:],
+                in_=grouped[:].rearrange("p g r t -> p (g r t)"),
+            )
+
+        def multiply(n, i):
+            product = products.tile([P, N_TILE], F32)
+            for g in range(PASSES):
+                tokens = slice(g * P, (g + 1) * P)
+                nc.tensor.matmul_mx(
+                    out=product[:],
+                    lhsT=x_codes[i][:, tokens].bitcast(FP8X4), lhsT_scale=x_scales[i][:, tokens],
+                    rhs=w_codes[n, g][:].bitcast(FP8X4), rhs_scale=w_scales[n, g][:],
+                    start=(g == 0), stop=(g == PASSES - 1),
+                )
+            return product
+
+        def store(out, first_head, i, result):
+            for r in range(ROWS):
+                nc.sync.dma_start(
+                    out=out[:, first_head : first_head + HEADS, ROWS * i + r, :], in_=result[r:P:ROWS, :, :]
+                )
+
+        def values(n, i):
+            product = multiply(n, i)
+            result = stage.tile([P, HEADS, HD], F32, name="value_result")
+            nc.vector.tensor_tensor(
+                out=result[:].rearrange("p h d -> p (h d)"), in0=product[:],
+                in1=bias[:, n * N_TILE : (n + 1) * N_TILE], op=ALU.add,
+            )
+            store(out_1, (n - KEY_CHUNKS) * HEADS, i, result)
+
+        def rotate_keys(n, i):
+            product = multiply(n, i)
+            halves = "p (h j e) -> p h e j"
+            keys = stage.tile([P, HEADS, 2, HP], F32)
+            nc.vector.tensor_tensor(
+                out=keys[:], in0=product[:].rearrange(halves, e=2, j=HP),
+                in1=bias[:, n * N_TILE : (n + 1) * N_TILE].rearrange(halves, e=2, j=HP), op=ALU.add,
+            )
+            key_squares = stage.tile([P, HEADS, HD], F32)
+            key_sum_sq = small.tile([P, HEADS], F32)
+            for h in range(HEADS):
+                nc.scalar.activation(
+                    out=key_squares[:, h, :], in_=keys[:, h].rearrange("p e j -> p (e j)"), func=ACT.Square,
+                    accum_out=key_sum_sq[:, h : h + 1],
+                )
+            key_inverse = inverse_rms(nc, small, minus_half, key_sum_sq, HD, HEADS, "k")
+
+            by_same = stage.tile([P, HEADS, 2, HP], F32)
+            by_cross = stage.tile([P, HEADS, 2, HP], F32)
+            every_head = [P, HEADS, 2, HP]
+            nc.vector.tensor_tensor(
+                out=by_same[:], in0=keys[:], in1=same[:, i].unsqueeze(1).to_broadcast(every_head), op=ALU.mult
+            )
+            nc.vector.tensor_tensor(
+                out=by_cross[:], in0=keys[:], in1=cross[:, i].unsqueeze(1).to_broadcast(every_head), op=ALU.mult
+            )
+            rotated = stage.tile([P, HEADS, 2, HP], F32)
+            for e in range(2):
+                nc.vector.tensor_tensor(
+                    out=rotated[:, :, e, :], in0=by_same[:, :, e, :], in1=by_cross[:, :, 1 - e, :], op=ALU.add
+                )
+            return rotated, key_inverse
+
+        def normalise_keys(n, i, rotated, key_inverse):
+            result = stage.tile([P, HEADS, HD], F32, name="key_result")
+            nc.vector.tensor_tensor(
+                out=result[:].rearrange("p h (j e) -> p h j e", e=2),
+                in0=rotated[:].rearrange("p h e j -> p h j e"),
+                in1=key_inverse[:].unsqueeze(2).unsqueeze(3).to_broadcast([P, HEADS, HP, 2]), op=ALU.mult,
+            )
+            store(out_0, n * HEADS, i, result)
+
+        for i in range(TOKEN_TILES):
+            token_norm(i)
+        for g in range(PASSES):
+            regroup(nc.vector.tensor_copy, 0, g)
+        for g in range(PASSES):
+            quantise(0, g)
+        for i in range(TOKEN_TILES):
+            turn_tokens(i)
+        for i in range(TOKEN_TILES):
+            quantise_tokens(i)
+        for n in range(1, KEY_CHUNKS):
+            for g in range(PASSES):
+                regroup(nc.scalar.copy, n, g)
+
+        key_pieces = [(n, i) for n in range(KEY_CHUNKS) for i in range(TOKEN_TILES)]
+        value_units = [(n, g) for n in range(KEY_CHUNKS, CHUNKS) for g in range(PASSES)]
+        assert len(key_pieces) == len(value_units)
+        waiting = None
+        for k, (n, i) in enumerate(key_pieces):
+            rotated, key_inverse = rotate_keys(n, i)
+            regroup(nc.scalar.copy, *value_units[k])
+            if k == 0:
+                for later in range(1, KEY_CHUNKS):
+                    for g in range(PASSES):
+                        quantise(later, g)
+            else:
+                normalise_keys(*waiting)
+                quantise(*value_units[k - 1])
+            waiting = (n, i, rotated, key_inverse)
+        normalise_keys(*waiting)
+        quantise(*value_units[-1])
+
+        for n in range(KEY_CHUNKS, CHUNKS):
+            for i in range(TOKEN_TILES):
+                values(n, i)

@@ -101,13 +101,11 @@ def rotation_tables(nc, keep, ln_w):
     return same, cross
 
 
-def inverse_rms(nc, small, minus_half, sum_sq, count, width, name):
-    mean_sq = small.tile([P, width], F32, name="mean_sq_" + name)
-    nc.gpsimd.tensor_scalar(
-        out=mean_sq[:], in0=sum_sq[:], scalar1=1.0 / count, scalar2=EPS, op0=ALU.mult, op1=ALU.add
-    )
+def inverse_rms(nc, small, sum_sq, count, width, name):
     inverse = small.tile([P, width], F32, name="inverse_" + name)
-    nc.gpsimd.tensor_tensor(out=inverse[:], in0=mean_sq[:], in1=minus_half[:, 0:width], op=ALU.pow)
+    nc.scalar.activation(
+        out=inverse[:], in_=sum_sq[:], func=ACT.Abs_reciprocal_sqrt, scale=1.0 / count, bias=EPS
+    )
     return inverse
 
 
@@ -140,8 +138,6 @@ def tile_attention_pb_kernel(tc, x, rmskv_w, kv_w, kv_b, ln_w, out_0, out_1):
                 nc.sync.dma_start(out=w_raw[n, g][:], in_=w_rows[g, :, :, n * N_TILE : (n + 1) * N_TILE])
 
         same, cross = rotation_tables(nc, keep, ln_w)
-        minus_half = keep.tile([P, HEADS], F32)
-        nc.gpsimd.memset(minus_half[:], -0.5)
         identity = keep.tile([P, P], F32)
         make_identity(nc, identity[:])
 
@@ -168,7 +164,7 @@ def tile_attention_pb_kernel(tc, x, rmskv_w, kv_w, kv_b, ln_w, out_0, out_1):
             squares = stage.tile([P, D], BF16)
             sum_sq = small.tile([P, 1], F32)
             nc.scalar.activation(out=squares[:], in_=x_sb[:, i, :], func=ACT.Square, accum_out=sum_sq[:])
-            x_inverse[i] = inverse_rms(nc, small, minus_half, sum_sq, D, 1, "x")
+            x_inverse[i] = inverse_rms(nc, small, sum_sq, D, 1, "x")
 
         def turn_tokens(i):
             scaled = stage.tile([P, PASSES, PACK, P], F32)
@@ -237,7 +233,7 @@ def tile_attention_pb_kernel(tc, x, rmskv_w, kv_w, kv_b, ln_w, out_0, out_1):
                     out=key_squares[:, h, :], in_=keys[:, h].rearrange("p e j -> p (e j)"), func=ACT.Square,
                     accum_out=key_sum_sq[:, h : h + 1],
                 )
-            key_inverse = inverse_rms(nc, small, minus_half, key_sum_sq, HD, HEADS, "k")
+            key_inverse = inverse_rms(nc, small, key_sum_sq, HD, HEADS, "k")
 
             by_same = stage.tile([P, HEADS, 2, HP], F32)
             by_cross = stage.tile([P, HEADS, 2, HP], F32)

@@ -38,20 +38,15 @@ FLOPS = 2 * B * CS * D * 2 * D
 BYTES = 2 * (B * CS * D + D * 2 * D + D + 2 * D + HD) + 4 * 2 * B * CS * D
 
 
-def angle_steps():
-    top = 1.0 + 4000.0 / 200.0
-    steps = []
-    for j in range(HP):
-        base = 200.0 * (top ** (j / (HP - 1)) - 1.0) / 1000.0
-        step = ST * base
-        steps.append(step - TWO_PI * round(step / TWO_PI))
-    return steps
-
-
-def rotation_tables(nc, keep, ln_w):
-    ln_gain = keep.tile([P, HD], BF16)
-    nc.scalar.dma_start(out=ln_gain[:], in_=ln_w.partition_broadcast(P))
-    gain_halves = ln_gain[:].rearrange("p (j e) -> p e j", e=2)
+def rotation_phases(nc, keep):
+    ratio = (1.0 + 4000.0 / 200.0) ** (1.0 / (HP - 1))
+    powers = keep.tile([P, HP], F32)
+    nc.vector.memset(powers[:, 0:1], 1.0)
+    for width in (1, 2, 4, 8, 16):
+        nc.vector.tensor_scalar_mul(out=powers[:, width : 2 * width], in0=powers[:, 0:width], scalar1=ratio**width)
+    steps = keep.tile([P, HP], F32)
+    scale = ST * 200.0 / 1000.0
+    nc.vector.tensor_scalar(out=steps[:], in0=powers[:], scalar1=scale, scalar2=-scale, op0=ALU.mult, op1=ALU.add)
 
     partition = keep.tile([P, 1], I32)
     nc.gpsimd.iota(partition[:], pattern=[[0, 1]], base=0, channel_multiplier=1)
@@ -63,8 +58,8 @@ def rotation_tables(nc, keep, ln_w):
         nc.vector.tensor_scalar_add(out=position[:, i : i + 1], in0=position[:, 0:1], scalar1=float(ROWS * i))
 
     phase = keep.tile([P, 2, TOKEN_TILES, HP], F32)
-    for j, step in enumerate(angle_steps()):
-        nc.vector.tensor_scalar_mul(out=phase[:, 0, :, j], in0=position[:], scalar1=step)
+    for i in range(TOKEN_TILES):
+        nc.vector.tensor_scalar_mul(out=phase[:, 0, i, :], in0=steps[:], scalar1=position[:, i : i + 1])
     nc.vector.tensor_scalar_add(out=phase[:, 1], in0=phase[:, 0], scalar1=0.5 * PI)
 
     turns = keep.tile([P, 2, TOKEN_TILES, HP], F32)
@@ -81,8 +76,11 @@ def rotation_tables(nc, keep, ln_w):
         out=phase[:].rearrange(flat), in0=turns[:].rearrange(flat), scalar=-TWO_PI_LOW,
         in1=phase[:].rearrange(flat), op0=ALU.mult, op1=ALU.add,
     )
-    sin_cos = keep.tile([P, 2, TOKEN_TILES, HP], F32)
-    nc.scalar.activation(out=sin_cos[:], in_=phase[:], func=ACT.Sin)
+    return phase
+
+
+def rotation_tables(nc, keep, sin_cos, ln_gain):
+    gain_halves = ln_gain[:].rearrange("p (j e) -> p e j", e=2)
     sin, cos = sin_cos[:, 0], sin_cos[:, 1]
 
     same = keep.tile([P, TOKEN_TILES, 2, HP], F32)
@@ -113,7 +111,7 @@ def tile_attention_pb_kernel(tc, x, rmskv_w, kv_w, kv_b, ln_w, out_0, out_1):
     nc = tc.nc
     with (
         tc.tile_pool(name="keep", bufs=1) as keep,
-        tc.tile_pool(name="stage", bufs=3) as stage,
+        tc.tile_pool(name="stage", bufs=4) as stage,
         tc.tile_pool(name="small", bufs=4) as small,
         tc.psum_pool(name="flipped", bufs=4) as flipped,
         tc.psum_pool(name="products", bufs=4) as products,
@@ -137,7 +135,17 @@ def tile_attention_pb_kernel(tc, x, rmskv_w, kv_w, kv_b, ln_w, out_0, out_1):
                 w_raw[n, g] = keep.tile([P, PACK, N_TILE], BF16, name="w_raw_%d_%d" % (n, g))
                 nc.sync.dma_start(out=w_raw[n, g][:], in_=w_rows[g, :, :, n * N_TILE : (n + 1) * N_TILE])
 
-        same, cross = rotation_tables(nc, keep, ln_w)
+        ln_gain = keep.tile([P, HD], BF16)
+        nc.scalar.dma_start(out=ln_gain[:], in_=ln_w.partition_broadcast(P))
+
+        def load_root_table():
+            nc.scalar.activation(out=warm[:], in_=one[:], func=ACT.Abs_reciprocal_sqrt)
+
+        one = keep.tile([P, 1], F32)
+        nc.vector.memset(one[:], 1.0)
+        warm = keep.tile([P, 1], F32)
+        load_root_table()
+        phase = rotation_phases(nc, keep)
         identity = keep.tile([P, P], F32)
         make_identity(nc, identity[:])
 
@@ -160,11 +168,15 @@ def tile_attention_pb_kernel(tc, x, rmskv_w, kv_w, kv_b, ln_w, out_0, out_1):
 
         x_inverse, x_turned, x_codes, x_scales = {}, {}, {}, {}
 
-        def token_norm(i):
+        x_sum_sq = {}
+
+        def token_squares(i):
             squares = stage.tile([P, D], BF16)
-            sum_sq = small.tile([P, 1], F32)
-            nc.scalar.activation(out=squares[:], in_=x_sb[:, i, :], func=ACT.Square, accum_out=sum_sq[:])
-            x_inverse[i] = inverse_rms(nc, small, sum_sq, D, 1, "x")
+            x_sum_sq[i] = small.tile([P, 1], F32, name="x_sum_sq")
+            nc.scalar.activation(out=squares[:], in_=x_sb[:, i, :], func=ACT.Square, accum_out=x_sum_sq[i][:])
+
+        def token_norm(i):
+            x_inverse[i] = inverse_rms(nc, small, x_sum_sq[i], D, 1, "x")
 
         def turn_tokens(i):
             scaled = stage.tile([P, PASSES, PACK, P], F32)
@@ -177,18 +189,22 @@ def tile_attention_pb_kernel(tc, x, rmskv_w, kv_w, kv_b, ln_w, out_0, out_1):
                 for t in range(PACK):
                     nc.tensor.transpose(x_turned[i, g][:, t, :], scaled[:, g, t, :], identity[:])
 
-        def quantise_tokens(i):
-            grouped = stage.tile([P, PASSES, P, PACK], BF16, name="x_grouped", align_bytes=64)
+        x_grouped = {}
+
+        def gain_tokens(i):
+            x_grouped[i] = stage.tile([P, PASSES, P, PACK], BF16, name="x_grouped", align_bytes=64)
             for g in range(PASSES):
                 nc.vector.tensor_tensor(
-                    out=grouped[:, g], in0=x_turned[i, g][:].rearrange("p t r -> p r t"),
+                    out=x_grouped[i][:, g], in0=x_turned[i, g][:].rearrange("p t r -> p r t"),
                     in1=rms_gain[:, g, :].unsqueeze(1).to_broadcast([P, P, PACK]), op=ALU.mult,
                 )
+
+        def quantise_tokens(i):
             x_codes[i] = keep.tile([P, PASSES * P], U32, name="x_codes_%d" % i, align_bytes=64)
             x_scales[i] = keep.tile([P, PASSES * P], U8, name="x_scales_%d" % i, align_bytes=64)
             nc.vector.quantize_mx(
                 out=x_codes[i][:].bitcast(FP8X4), scales=x_scales[i][:],
-                in_=grouped[:].rearrange("p g r t -> p (g r t)"),
+                in_=x_grouped[i][:].rearrange("p g r t -> p (g r t)"),
             )
 
         def multiply(n, i):
@@ -218,48 +234,58 @@ def tile_attention_pb_kernel(tc, x, rmskv_w, kv_w, kv_b, ln_w, out_0, out_1):
             )
             store(out_1, (n - KEY_CHUNKS) * HEADS, i, result)
 
-        def rotate_keys(n, i):
+        keys, key_inverse, by_same, by_cross, rotated = {}, {}, {}, {}, {}
+        every_head = [P, HEADS, 2, HP]
+
+        def biased_keys(n, i):
             product = multiply(n, i)
             halves = "p (h j e) -> p h e j"
-            keys = stage.tile([P, HEADS, 2, HP], F32)
+            keys[i] = stage.tile([P, HEADS, 2, HP], F32, name="keys")
             nc.vector.tensor_tensor(
-                out=keys[:], in0=product[:].rearrange(halves, e=2, j=HP),
+                out=keys[i][:], in0=product[:].rearrange(halves, e=2, j=HP),
                 in1=bias[:, n * N_TILE : (n + 1) * N_TILE].rearrange(halves, e=2, j=HP), op=ALU.add,
             )
+
+        def key_norm(n, i):
             key_squares = stage.tile([P, HEADS, HD], F32)
             key_sum_sq = small.tile([P, HEADS], F32)
             for h in range(HEADS):
                 nc.scalar.activation(
-                    out=key_squares[:, h, :], in_=keys[:, h].rearrange("p e j -> p (e j)"), func=ACT.Square,
+                    out=key_squares[:, h, :], in_=keys[i][:, h].rearrange("p e j -> p (e j)"), func=ACT.Square,
                     accum_out=key_sum_sq[:, h : h + 1],
                 )
-            key_inverse = inverse_rms(nc, small, key_sum_sq, HD, HEADS, "k")
+            key_inverse[n, i] = inverse_rms(nc, small, key_sum_sq, HD, HEADS, "k")
 
-            by_same = stage.tile([P, HEADS, 2, HP], F32)
-            by_cross = stage.tile([P, HEADS, 2, HP], F32)
-            every_head = [P, HEADS, 2, HP]
+        def times_same(i):
+            by_same[i] = stage.tile(every_head, F32, name="by_same")
             nc.vector.tensor_tensor(
-                out=by_same[:], in0=keys[:], in1=same[:, i].unsqueeze(1).to_broadcast(every_head), op=ALU.mult
+                out=by_same[i][:], in0=keys[i][:], in1=same[:, i].unsqueeze(1).to_broadcast(every_head), op=ALU.mult
             )
+
+        def times_cross(i):
+            by_cross[i] = stage.tile(every_head, F32, name="by_cross")
             nc.vector.tensor_tensor(
-                out=by_cross[:], in0=keys[:], in1=cross[:, i].unsqueeze(1).to_broadcast(every_head), op=ALU.mult
+                out=by_cross[i][:], in0=keys[i][:], in1=cross[:, i].unsqueeze(1).to_broadcast(every_head), op=ALU.mult
             )
-            rotated = stage.tile([P, HEADS, 2, HP], F32)
+
+        def add_halves(n, i):
+            rotated[n, i] = stage.tile(every_head, F32, name="rotated")
             for e in range(2):
                 nc.vector.tensor_tensor(
-                    out=rotated[:, :, e, :], in0=by_same[:, :, e, :], in1=by_cross[:, :, 1 - e, :], op=ALU.add
+                    out=rotated[n, i][:, :, e, :], in0=by_same[i][:, :, e, :], in1=by_cross[i][:, :, 1 - e, :], op=ALU.add
                 )
-            return rotated, key_inverse
 
-        def normalise_keys(n, i, rotated, key_inverse):
+        def normalise_keys(n, i):
             result = stage.tile([P, HEADS, HD], F32, name="key_result")
             nc.vector.tensor_tensor(
                 out=result[:].rearrange("p h (j e) -> p h j e", e=2),
-                in0=rotated[:].rearrange("p h e j -> p h j e"),
-                in1=key_inverse[:].unsqueeze(2).unsqueeze(3).to_broadcast([P, HEADS, HP, 2]), op=ALU.mult,
+                in0=rotated[n, i][:].rearrange("p h e j -> p h j e"),
+                in1=key_inverse[n, i][:].unsqueeze(2).unsqueeze(3).to_broadcast([P, HEADS, HP, 2]), op=ALU.mult,
             )
             store(out_0, n * HEADS, i, result)
 
+        for i in range(TOKEN_TILES):
+            token_squares(i)
         for i in range(TOKEN_TILES):
             token_norm(i)
         for g in range(PASSES):
@@ -268,29 +294,41 @@ def tile_attention_pb_kernel(tc, x, rmskv_w, kv_w, kv_b, ln_w, out_0, out_1):
             quantise(0, g)
         for i in range(TOKEN_TILES):
             turn_tokens(i)
+        sin_cos = keep.tile([P, 2, TOKEN_TILES, HP], F32)
+        nc.scalar.activation(out=sin_cos[:], in_=phase[:], func=ACT.Sin)
+        load_root_table()
+        for i in range(TOKEN_TILES):
+            gain_tokens(i)
         for i in range(TOKEN_TILES):
             quantise_tokens(i)
+        same, cross = rotation_tables(nc, keep, sin_cos, ln_gain)
         for n in range(1, KEY_CHUNKS):
             for g in range(PASSES):
                 regroup(nc.scalar.copy, n, g)
 
-        key_pieces = [(n, i) for n in range(KEY_CHUNKS) for i in range(TOKEN_TILES)]
-        value_units = [(n, g) for n in range(KEY_CHUNKS, CHUNKS) for g in range(PASSES)]
-        assert len(key_pieces) == len(value_units)
-        waiting = None
-        for k, (n, i) in enumerate(key_pieces):
-            rotated, key_inverse = rotate_keys(n, i)
-            regroup(nc.scalar.copy, *value_units[k])
-            if k == 0:
-                for later in range(1, KEY_CHUNKS):
-                    for g in range(PASSES):
-                        quantise(later, g)
-            else:
-                normalise_keys(*waiting)
-                quantise(*value_units[k - 1])
-            waiting = (n, i, rotated, key_inverse)
-        normalise_keys(*waiting)
-        quantise(*value_units[-1])
+        tiles = range(TOKEN_TILES)
+        for n in range(KEY_CHUNKS):
+            for i in tiles:
+                biased_keys(n, i)
+            for i in tiles:
+                key_norm(n, i)
+            for g in range(PASSES):
+                regroup(nc.scalar.copy, KEY_CHUNKS + n, g)
+            if n > 0:
+                for i in tiles:
+                    normalise_keys(n - 1, i)
+            for i in tiles:
+                times_same(i)
+            for i in tiles:
+                times_cross(i)
+            for i in tiles:
+                add_halves(n, i)
+            for g in range(PASSES):
+                quantise(n + 1, g)
+        for i in tiles:
+            normalise_keys(KEY_CHUNKS - 1, i)
+        for g in range(PASSES):
+            quantise(CHUNKS - 1, g)
 
         for n in range(KEY_CHUNKS, CHUNKS):
             for i in range(TOKEN_TILES):

@@ -307,13 +307,15 @@ def tile_attention_pb_kernel(tc, x, rmskv_w, kv_w, kv_b, ln_w, out_0, out_1):
                 regroup(nc.scalar.copy, n, g)
 
         tiles = range(TOKEN_TILES)
+        last_unit = (CHUNKS - 1, PASSES - 1)
         for n in range(KEY_CHUNKS):
             for i in tiles:
                 biased_keys(n, i)
             for i in tiles:
                 key_norm(n, i)
             for g in range(PASSES):
-                regroup(nc.scalar.copy, KEY_CHUNKS + n, g)
+                if (KEY_CHUNKS + n, g) != last_unit:
+                    regroup(nc.scalar.copy, KEY_CHUNKS + n, g)
             if n > 0:
                 for i in tiles:
                     normalise_keys(n - 1, i)
@@ -325,11 +327,13 @@ def tile_attention_pb_kernel(tc, x, rmskv_w, kv_w, kv_b, ln_w, out_0, out_1):
                 add_halves(n, i)
             for g in range(PASSES):
                 quantise(n + 1, g)
+            if n == 0:
+                regroup(nc.vector.tensor_copy, *last_unit)
         for i in tiles:
             normalise_keys(KEY_CHUNKS - 1, i)
-        for g in range(PASSES):
-            quantise(CHUNKS - 1, g)
-
         for n in range(KEY_CHUNKS, CHUNKS):
-            for i in range(TOKEN_TILES):
+            if n == CHUNKS - 1:
+                for g in range(PASSES):
+                    quantise(n, g)
+            for i in tiles:
                 values(n, i)

@@ -38,45 +38,55 @@ FLOPS = 2 * B * CS * D * 2 * D
 BYTES = 2 * (B * CS * D + D * 2 * D + D + 2 * D + HD) + 4 * 2 * B * CS * D
 
 
-def rotation_phases(nc, keep):
+def rotation_phases(nc, keep, one):
     ratio = (1.0 + 4000.0 / 200.0) ** (1.0 / (HP - 1))
-    powers = keep.tile([P, HP], F32)
-    nc.vector.memset(powers[:, 0:1], 1.0)
-    for width in (1, 2, 4, 8, 16):
-        nc.vector.tensor_scalar_mul(out=powers[:, width : 2 * width], in0=powers[:, 0:width], scalar1=ratio**width)
-    steps = keep.tile([P, HP], F32)
     scale = ST * 200.0 / 1000.0
-    nc.vector.tensor_scalar(out=steps[:], in0=powers[:], scalar1=scale, scalar2=-scale, op0=ALU.mult, op1=ALU.add)
-
+    powers = keep.tile([P, HP], F32)
+    for j in range(8):
+        nc.vector.tensor_scalar_mul(out=powers[:, j : j + 1], in0=one[:], scalar1=ratio**j)
     partition = keep.tile([P, 1], I32)
     nc.gpsimd.iota(partition[:], pattern=[[0, 1]], base=0, channel_multiplier=1)
     row = keep.tile([P, 1], I32)
     nc.vector.tensor_single_scalar(out=row[:], in_=partition[:], scalar=ROWS - 1, op=ALU.bitwise_and)
-    position = keep.tile([P, TOKEN_TILES], F32)
-    nc.vector.tensor_copy(out=position[:, 0:1], in_=row[:])
-    for i in range(1, TOKEN_TILES):
-        nc.vector.tensor_scalar_add(out=position[:, i : i + 1], in0=position[:, 0:1], scalar1=float(ROWS * i))
-
-    phase = keep.tile([P, 2, TOKEN_TILES, HP], F32)
+    nc.vector.tensor_scalar_mul(out=powers[:, 8:16], in0=powers[:, 0:8], scalar1=ratio**8)
+    turn_by = keep.tile([P, TOKEN_TILES], F32)
+    offset = keep.tile([P, 2, TOKEN_TILES], F32)
     for i in range(TOKEN_TILES):
-        nc.vector.tensor_scalar_mul(out=phase[:, 0, i, :], in0=steps[:], scalar1=position[:, i : i + 1])
-    nc.vector.tensor_scalar_add(out=phase[:, 1], in0=phase[:, 0], scalar1=0.5 * PI)
+        nc.vector.tensor_scalar(
+            out=turn_by[:, i : i + 1], in0=row[:], scalar1=scale, scalar2=scale * ROWS * i, op0=ALU.mult, op1=ALU.add
+        )
+        for a in range(2):
+            nc.vector.tensor_scalar(
+                out=offset[:, a, i : i + 1], in0=row[:], scalar1=-scale, scalar2=a * 0.5 * PI - scale * ROWS * i,
+                op0=ALU.mult, op1=ALU.add,
+            )
+    nc.vector.tensor_scalar_mul(out=powers[:, 16:32], in0=powers[:, 0:16], scalar1=ratio**16)
+    phase = keep.tile([P, 2, TOKEN_TILES, HP], F32)
+    for a in range(2):
+        for i in range(TOKEN_TILES):
+            nc.vector.tensor_scalar(
+                out=phase[:, a, i, :], in0=powers[:], scalar1=turn_by[:, i : i + 1], scalar2=offset[:, a, i : i + 1],
+                op0=ALU.mult, op1=ALU.add,
+            )
 
     turns = keep.tile([P, 2, TOKEN_TILES, HP], F32)
-    nc.vector.tensor_scalar(
-        out=turns[:], in0=phase[:], scalar1=1.0 / TWO_PI, scalar2=ROUND_TO_INTEGER, op0=ALU.mult, op1=ALU.add
-    )
-    nc.vector.tensor_scalar_sub(out=turns[:], in0=turns[:], scalar1=ROUND_TO_INTEGER)
     flat = "p a i j -> p (a i j)"
-    nc.vector.scalar_tensor_tensor(
-        out=phase[:].rearrange(flat), in0=turns[:].rearrange(flat), scalar=-TWO_PI_HIGH,
-        in1=phase[:].rearrange(flat), op0=ALU.mult, op1=ALU.add,
-    )
-    nc.vector.scalar_tensor_tensor(
-        out=phase[:].rearrange(flat), in0=turns[:].rearrange(flat), scalar=-TWO_PI_LOW,
-        in1=phase[:].rearrange(flat), op0=ALU.mult, op1=ALU.add,
-    )
-    return phase
+
+    def subtract_turns(part_of_two_pi):
+        nc.vector.scalar_tensor_tensor(
+            out=phase[:].rearrange(flat), in0=turns[:].rearrange(flat), scalar=-part_of_two_pi,
+            in1=phase[:].rearrange(flat), op0=ALU.mult, op1=ALU.add,
+        )
+
+    last_steps = [
+        lambda: nc.vector.tensor_scalar(
+            out=turns[:], in0=phase[:], scalar1=1.0 / TWO_PI, scalar2=ROUND_TO_INTEGER, op0=ALU.mult, op1=ALU.add
+        ),
+        lambda: nc.vector.tensor_scalar_sub(out=turns[:], in0=turns[:], scalar1=ROUND_TO_INTEGER),
+        lambda: subtract_turns(TWO_PI_HIGH),
+        lambda: subtract_turns(TWO_PI_LOW),
+    ]
+    return phase, last_steps
 
 
 def rotation_tables(nc, keep, sin_cos, ln_gain):
@@ -145,7 +155,7 @@ def tile_attention_pb_kernel(tc, x, rmskv_w, kv_w, kv_b, ln_w, out_0, out_1):
         nc.vector.memset(one[:], 1.0)
         warm = keep.tile([P, 1], F32)
         load_root_table()
-        phase = rotation_phases(nc, keep)
+        phase, last_steps = rotation_phases(nc, keep, one)
         identity = keep.tile([P, P], F32)
         make_identity(nc, identity[:])
 
@@ -234,7 +244,7 @@ def tile_attention_pb_kernel(tc, x, rmskv_w, kv_w, kv_b, ln_w, out_0, out_1):
             )
             store(out_1, (n - KEY_CHUNKS) * HEADS, i, result)
 
-        keys, key_inverse, by_same, by_cross, rotated = {}, {}, {}, {}, {}
+        keys, key_sum_sq, key_inverse, by_same, by_cross, rotated = {}, {}, {}, {}, {}, {}
         every_head = [P, HEADS, 2, HP]
 
         def biased_keys(n, i):
@@ -248,13 +258,15 @@ def tile_attention_pb_kernel(tc, x, rmskv_w, kv_w, kv_b, ln_w, out_0, out_1):
 
         def key_norm(n, i):
             key_squares = stage.tile([P, HEADS, HD], F32)
-            key_sum_sq = small.tile([P, HEADS], F32)
+            key_sum_sq[i] = small.tile([P, HEADS], F32, name="key_sum_sq")
             for h in range(HEADS):
                 nc.scalar.activation(
                     out=key_squares[:, h, :], in_=keys[i][:, h].rearrange("p e j -> p (e j)"), func=ACT.Square,
-                    accum_out=key_sum_sq[:, h : h + 1],
+                    accum_out=key_sum_sq[i][:, h : h + 1],
                 )
-            key_inverse[n, i] = inverse_rms(nc, small, key_sum_sq, HD, HEADS, "k")
+
+        def key_root(n, i):
+            key_inverse[n, i] = inverse_rms(nc, small, key_sum_sq[i], HD, HEADS, "k")
 
         def times_same(i):
             by_same[i] = stage.tile(every_head, F32, name="by_same")
@@ -290,8 +302,10 @@ def tile_attention_pb_kernel(tc, x, rmskv_w, kv_w, kv_b, ln_w, out_0, out_1):
             token_norm(i)
         for g in range(PASSES):
             regroup(nc.vector.tensor_copy, 0, g)
+            last_steps[g]()
         for g in range(PASSES):
             quantise(0, g)
+            last_steps[PASSES + g]()
         for i in range(TOKEN_TILES):
             turn_tokens(i)
         sin_cos = keep.tile([P, 2, TOKEN_TILES, HP], F32)
@@ -316,6 +330,8 @@ def tile_attention_pb_kernel(tc, x, rmskv_w, kv_w, kv_b, ln_w, out_0, out_1):
             for g in range(PASSES):
                 if (KEY_CHUNKS + n, g) != last_unit:
                     regroup(nc.scalar.copy, KEY_CHUNKS + n, g)
+            for i in tiles:
+                key_root(n, i)
             if n > 0:
                 for i in tiles:
                     normalise_keys(n - 1, i)

@@ -139,8 +139,9 @@ def tile_attention_pb_kernel(tc, x, rmskv_w, kv_w, kv_b, ln_w, out_0, out_1):
         w_rows = kv_w.rearrange("(g p t) n -> g p t n", g=PASSES, t=PACK)
         w_raw = {}
         for n in range(CHUNKS):
-            if n == KEY_CHUNKS:
-                nc.sync.dma_start(out=bias[:], in_=kv_b.partition_broadcast(P))
+            if 0 < n <= 2:
+                half = slice((n - 1) * D, n * D)
+                nc.sync.dma_start(out=bias[:, half], in_=kv_b[half].partition_broadcast(P))
             for g in range(PASSES):
                 w_raw[n, g] = keep.tile([P, PACK, N_TILE], BF16, name="w_raw_%d_%d" % (n, g))
                 nc.sync.dma_start(out=w_raw[n, g][:], in_=w_rows[g, :, :, n * N_TILE : (n + 1) * N_TILE])
@@ -327,11 +328,11 @@ def tile_attention_pb_kernel(tc, x, rmskv_w, kv_w, kv_b, ln_w, out_0, out_1):
                 biased_keys(n, i)
             for i in tiles:
                 key_norm(n, i)
+            for i in tiles:
+                key_root(n, i)
             for g in range(PASSES):
                 if (KEY_CHUNKS + n, g) != last_unit:
                     regroup(nc.scalar.copy, KEY_CHUNKS + n, g)
-            for i in tiles:
-                key_root(n, i)
             if n > 0:
                 for i in tiles:
                     normalise_keys(n - 1, i)

@@ -132,8 +132,9 @@ def tile_attention_pb_kernel(tc, x, rmskv_w, kv_w, kv_b, ln_w, out_0, out_1):
         for r in range(ROWS):
             nc.sync.dma_start(out=x_sb[r:P:ROWS, :, :], in_=x_rows[r, 0])
 
-        rms_gain = keep.tile([P, PASSES, PACK], BF16)
-        nc.scalar.dma_start(out=rms_gain[:], in_=rmskv_w.rearrange("(g p t) -> p g t", g=PASSES, t=PACK))
+        gain_row = keep.tile([P, D], BF16)
+        nc.vector.memset(gain_row[:], 0.0)
+        nc.scalar.dma_start(out=gain_row[0:1, :], in_=rmskv_w.rearrange("(o f) -> o f", o=1))
 
         bias = keep.tile([P, 2 * D], BF16)
         w_rows = kv_w.rearrange("(g p t) n -> g p t n", g=PASSES, t=PACK)
@@ -189,26 +190,41 @@ def tile_attention_pb_kernel(tc, x, rmskv_w, kv_w, kv_b, ln_w, out_0, out_1):
         def token_norm(i):
             x_inverse[i] = inverse_rms(nc, small, x_sum_sq[i], D, 1, "x")
 
-        def turn_tokens(i):
-            scaled = stage.tile([P, PASSES, PACK, P], F32)
-            nc.scalar.activation(
-                out=scaled[:], in_=x_sb[:, i, :].rearrange("p (g q t) -> p g t q", g=PASSES, t=PACK),
-                func=ACT.Copy, scale=x_inverse[i][:, 0:1],
+        ones = keep.tile([P, P], BF16)
+        nc.vector.memset(ones[:], 1.0)
+        gain_all = {}
+        for g in range(PASSES):
+            gain_all[g] = products.tile([P, K_PASS], F32, name="product")
+            nc.tensor.matmul(
+                out=gain_all[g][:], lhsT=ones[:], rhs=gain_row[:, g * K_PASS : (g + 1) * K_PASS], start=True, stop=True
             )
-            for g in range(PASSES):
-                x_turned[i, g] = flipped.tile([P, PACK, P], F32, name="turned")
-                for t in range(PACK):
-                    nc.tensor.transpose(x_turned[i, g][:, t, :], scaled[:, g, t, :], identity[:])
 
-        x_grouped = {}
+        x_normed, x_grouped = {}, {}
 
-        def gain_tokens(i):
-            x_grouped[i] = stage.tile([P, PASSES, P, PACK], BF16, name="x_grouped", align_bytes=64)
+        def norm_tokens(i, short_steps):
+            x_normed[i] = stage.tile([P, D], BF16, name="x_normed")
             for g in range(PASSES):
-                nc.vector.tensor_tensor(
-                    out=x_grouped[i][:, g], in0=x_turned[i, g][:].rearrange("p t r -> p r t"),
-                    in1=rms_gain[:, g, :].unsqueeze(1).to_broadcast([P, P, PACK]), op=ALU.mult,
+                features = slice(g * K_PASS, (g + 1) * K_PASS)
+                nc.vector.scalar_tensor_tensor(
+                    out=x_normed[i][:, features], in0=x_sb[:, i, features], scalar=x_inverse[i][:, 0:1],
+                    in1=gain_all[g][:], op0=ALU.mult, op1=ALU.mult,
                 )
+                for step in short_steps[g : g + 1]:
+                    step()
+
+        def turn_tokens(i):
+            words = x_normed[i][:].bitcast(F32)
+            words_of_pass = K_PASS // 2
+            x_turned[i] = flipped.tile([P, PASSES, 2, P], F32, name="turned")
+            for g in range(PASSES):
+                for u in range(2):
+                    nc.tensor.transpose(
+                        x_turned[i][:, g, u, :], words[:, g * words_of_pass + u : (g + 1) * words_of_pass : 2], identity[:]
+                    )
+
+        def gather_tokens(i):
+            x_grouped[i] = stage.tile([P, PASSES, P, PACK], BF16, name="x_grouped", align_bytes=64)
+            nc.scalar.copy(out=x_grouped[i][:].bitcast(F32), in_=x_turned[i][:].rearrange("p g u r -> p g r u"))
 
         def quantise_tokens(i):
             x_codes[i] = keep.tile([P, PASSES * P], U32, name="x_codes_%d" % i, align_bytes=64)
@@ -301,21 +317,21 @@ def tile_attention_pb_kernel(tc, x, rmskv_w, kv_w, kv_b, ln_w, out_0, out_1):
             token_squares(i)
         for i in range(TOKEN_TILES):
             token_norm(i)
-        for g in range(PASSES):
-            regroup(nc.vector.tensor_copy, 0, g)
-            last_steps[g]()
-        for g in range(PASSES):
-            quantise(0, g)
-            last_steps[PASSES + g]()
+        regroup(nc.vector.tensor_copy, 0, 0)
+        last_steps[0]()
         for i in range(TOKEN_TILES):
+            norm_tokens(i, last_steps[1 + 2 * i :  3 + 2 * i])
             turn_tokens(i)
         sin_cos = keep.tile([P, 2, TOKEN_TILES, HP], F32)
         nc.scalar.activation(out=sin_cos[:], in_=phase[:], func=ACT.Sin)
+        for i in range(TOKEN_TILES):
+            gather_tokens(i)
         load_root_table()
-        for i in range(TOKEN_TILES):
-            gain_tokens(i)
-        for i in range(TOKEN_TILES):
-            quantise_tokens(i)
+        regroup(nc.vector.tensor_copy, 0, 1)
+        quantise(0, 0)
+        quantise_tokens(0)
+        quantise(0, 1)
+        quantise_tokens(1)
         same, cross = rotation_tables(nc, keep, sin_cos, ln_gain)
         for n in range(1, KEY_CHUNKS):
             for g in range(PASSES):
@@ -333,9 +349,6 @@ def tile_attention_pb_kernel(tc, x, rmskv_w, kv_w, kv_b, ln_w, out_0, out_1):
             for g in range(PASSES):
                 if (KEY_CHUNKS + n, g) != last_unit:
                     regroup(nc.scalar.copy, KEY_CHUNKS + n, g)
-            if n > 0:
-                for i in tiles:
-                    normalise_keys(n - 1, i)
             for i in tiles:
                 times_same(i)
             for i in tiles:
@@ -346,8 +359,8 @@ def tile_attention_pb_kernel(tc, x, rmskv_w, kv_w, kv_b, ln_w, out_0, out_1):
                 quantise(n + 1, g)
             if n == 0:
                 regroup(nc.vector.tensor_copy, *last_unit)
-        for i in tiles:
-            normalise_keys(KEY_CHUNKS - 1, i)
+            for i in tiles:
+                normalise_keys(n, i)
         for n in range(KEY_CHUNKS, CHUNKS):
             if n == CHUNKS - 1:
                 for g in range(PASSES):

@@ -313,6 +313,16 @@ def tile_attention_pb_kernel(tc, x, rmskv_w, kv_w, kv_b, ln_w, out_0, out_1):
             )
             store(out_0, n * HEADS, i, result)
 
+        def normalise_keys_on_scalar(n, i):
+            result = stage.tile([P, HEADS, HD], F32, name="key_result")
+            for h in range(HEADS):
+                nc.scalar.activation(
+                    out=result[:, h, :].rearrange("p (j e) -> p j e", e=2),
+                    in_=rotated[n, i][:, h].rearrange("p e j -> p j e"),
+                    func=ACT.Copy, scale=key_inverse[n, i][:, h : h + 1],
+                )
+            store(out_0, n * HEADS, i, result)
+
         for i in range(TOKEN_TILES):
             token_squares(i)
         for i in range(TOKEN_TILES):
@@ -332,13 +342,11 @@ def tile_attention_pb_kernel(tc, x, rmskv_w, kv_w, kv_b, ln_w, out_0, out_1):
         quantise_tokens(0)
         quantise(0, 1)
         quantise_tokens(1)
+        regroup(nc.vector.tensor_copy, 1, 0)
         same, cross = rotation_tables(nc, keep, sin_cos, ln_gain)
-        for n in range(1, KEY_CHUNKS):
-            for g in range(PASSES):
-                regroup(nc.scalar.copy, n, g)
+        regroup(nc.scalar.copy, 1, 1)
 
         tiles = range(TOKEN_TILES)
-        last_unit = (CHUNKS - 1, PASSES - 1)
         for n in range(KEY_CHUNKS):
             for i in tiles:
                 biased_keys(n, i)
@@ -347,20 +355,23 @@ def tile_attention_pb_kernel(tc, x, rmskv_w, kv_w, kv_b, ln_w, out_0, out_1):
             for i in tiles:
                 key_root(n, i)
             for g in range(PASSES):
-                if (KEY_CHUNKS + n, g) != last_unit:
-                    regroup(nc.scalar.copy, KEY_CHUNKS + n, g)
+                regroup(nc.scalar.copy, KEY_CHUNKS + n, g)
             for i in tiles:
                 times_same(i)
+            if n == 0:
+                for g in range(PASSES):
+                    quantise(1, g)
             for i in tiles:
                 times_cross(i)
             for i in tiles:
                 add_halves(n, i)
-            for g in range(PASSES):
-                quantise(n + 1, g)
             if n == 0:
-                regroup(nc.vector.tensor_copy, *last_unit)
-            for i in tiles:
-                normalise_keys(n, i)
+                for i in tiles:
+                    normalise_keys_on_scalar(n, i)
+        for g in range(PASSES):
+            quantise(KEY_CHUNKS, g)
+        for i in tiles:
+            normalise_keys(KEY_CHUNKS - 1, i)
         for n in range(KEY_CHUNKS, CHUNKS):
             if n == CHUNKS - 1:
                 for g in range(PASSES):

@@ -234,32 +234,34 @@ def tile_attention_pb_kernel(tc, x, rmskv_w, kv_w, kv_b, ln_w, out_0, out_1):
                 in_=x_grouped[i][:].rearrange("p g r t -> p (g r t)"),
             )
 
+        def multiply_pass(n, i, g, product):
+            tokens = slice(g * P, (g + 1) * P)
+            nc.tensor.matmul_mx(
+                out=product[:],
+                lhsT=x_codes[i][:, tokens].bitcast(FP8X4), lhsT_scale=x_scales[i][:, tokens],
+                rhs=w_codes[n, g][:].bitcast(FP8X4), rhs_scale=w_scales[n, g][:],
+                start=(g == 0), stop=(g == PASSES - 1),
+            )
+
         def multiply(n, i):
-            product = products.tile([P, N_TILE], F32)
+            product = products.tile([P, N_TILE], F32, name="product")
             for g in range(PASSES):
-                tokens = slice(g * P, (g + 1) * P)
-                nc.tensor.matmul_mx(
-                    out=product[:],
-                    lhsT=x_codes[i][:, tokens].bitcast(FP8X4), lhsT_scale=x_scales[i][:, tokens],
-                    rhs=w_codes[n, g][:].bitcast(FP8X4), rhs_scale=w_scales[n, g][:],
-                    start=(g == 0), stop=(g == PASSES - 1),
-                )
+                multiply_pass(n, i, g, product)
             return product
 
-        def store(out, first_head, i, result):
+        def store(out, first_head, i, result, queues=(nc.sync,)):
             for r in range(ROWS):
-                nc.sync.dma_start(
+                queues[r % len(queues)].dma_start(
                     out=out[:, first_head : first_head + HEADS, ROWS * i + r, :], in_=result[r:P:ROWS, :, :]
                 )
 
-        def values(n, i):
-            product = multiply(n, i)
+        def values(n, i, product, queues=(nc.sync,)):
             result = stage.tile([P, HEADS, HD], F32, name="value_result")
             nc.vector.tensor_tensor(
                 out=result[:].rearrange("p h d -> p (h d)"), in0=product[:],
                 in1=bias[:, n * N_TILE : (n + 1) * N_TILE], op=ALU.add,
             )
-            store(out_1, (n - KEY_CHUNKS) * HEADS, i, result)
+            store(out_1, (n - KEY_CHUNKS) * HEADS, i, result, queues)
 
         keys, key_sum_sq, key_inverse, by_same, by_cross, rotated = {}, {}, {}, {}, {}, {}
         every_head = [P, HEADS, 2, HP]
@@ -313,16 +315,6 @@ def tile_attention_pb_kernel(tc, x, rmskv_w, kv_w, kv_b, ln_w, out_0, out_1):
             )
             store(out_0, n * HEADS, i, result)
 
-        def normalise_keys_on_scalar(n, i):
-            result = stage.tile([P, HEADS, HD], F32, name="key_result")
-            for h in range(HEADS):
-                nc.scalar.activation(
-                    out=result[:, h, :].rearrange("p (j e) -> p j e", e=2),
-                    in_=rotated[n, i][:, h].rearrange("p e j -> p j e"),
-                    func=ACT.Copy, scale=key_inverse[n, i][:, h : h + 1],
-                )
-            store(out_0, n * HEADS, i, result)
-
         for i in range(TOKEN_TILES):
             token_squares(i)
         for i in range(TOKEN_TILES):
@@ -347,34 +339,53 @@ def tile_attention_pb_kernel(tc, x, rmskv_w, kv_w, kv_b, ln_w, out_0, out_1):
         regroup(nc.scalar.copy, 1, 1)
 
         tiles = range(TOKEN_TILES)
-        for n in range(KEY_CHUNKS):
-            for i in tiles:
-                biased_keys(n, i)
-            for i in tiles:
-                key_norm(n, i)
-            for i in tiles:
-                key_root(n, i)
-            for g in range(PASSES):
-                regroup(nc.scalar.copy, KEY_CHUNKS + n, g)
-            for i in tiles:
-                times_same(i)
-            if n == 0:
-                for g in range(PASSES):
-                    quantise(1, g)
-            for i in tiles:
-                times_cross(i)
-            for i in tiles:
-                add_halves(n, i)
-            if n == 0:
-                for i in tiles:
-                    normalise_keys_on_scalar(n, i)
-        for g in range(PASSES):
-            quantise(KEY_CHUNKS, g)
+        passes = range(PASSES)
+        first_values, last = KEY_CHUNKS, CHUNKS - 1
         for i in tiles:
-            normalise_keys(KEY_CHUNKS - 1, i)
-        for n in range(KEY_CHUNKS, CHUNKS):
-            if n == CHUNKS - 1:
-                for g in range(PASSES):
-                    quantise(n, g)
-            for i in tiles:
-                values(n, i)
+            biased_keys(0, i)
+        for i in tiles:
+            key_norm(0, i)
+        for i in tiles:
+            key_root(0, i)
+        for g in passes:
+            regroup(nc.scalar.copy, first_values, g)
+        for i in tiles:
+            times_same(i)
+        for g in passes:
+            quantise(1, g)
+        for i in tiles:
+            times_cross(i)
+        for i in tiles:
+            add_halves(0, i)
+        for i in tiles:
+            normalise_keys(0, i)
+        for i in tiles:
+            biased_keys(1, i)
+        for i in tiles:
+            key_norm(1, i)
+        for i in tiles:
+            key_root(1, i)
+        for g in passes:
+            regroup(nc.scalar.copy, last, g)
+        for g in passes:
+            quantise(first_values, g)
+        value_products = [multiply(first_values, i) for i in tiles]
+        for i in tiles:
+            times_same(i)
+        for i in tiles:
+            times_cross(i)
+        for i in tiles:
+            values(first_values, i, value_products[i])
+        for i in tiles:
+            add_halves(1, i)
+        last_products = [products.tile([P, N_TILE], F32, name="product") for i in tiles]
+        quantise(last, 0)
+        for i in tiles:
+            multiply_pass(last, i, 0, last_products[i])
+        for i in tiles:
+            normalise_keys(1, i)
+        quantise(last, 1)
+        for i in tiles:
+            multiply_pass(last, i, 1, last_products[i])
+        for i in tiles:
+            values(last, i, last_products[i])

@@ -9,7 +9,6 @@ U8 = mybir.dt.uint8
 FP8X4 = mybir.dt.float8_e4m3fn_x4
 ALU = mybir.AluOpType
 ACT = mybir.ActivationFunctionType
-AXIS = mybir.AxisListType
 
 B, C, D, H, ST = 32, 32, 1024, 16, 4
 HD = D // H
@@ -24,9 +23,14 @@ PASSES = D // K_PASS
 TOKEN_TILES = B * CS // P
 ROWS = P // B
 N_TILE = 512
+TOKENS = TOKEN_TILES * P
 CHUNKS = 2 * D // N_TILE
 KEY_CHUNKS = D // N_TILE
 HEADS = N_TILE // HD
+KEY_TILES = D // P
+TILES_OF_CHUNK = N_TILE // P
+HEADS_OF_TILE = P // HD
+LN_ROW = 32
 
 PI = 3.141592653589793
 TWO_PI = 2.0 * PI
@@ -39,82 +43,51 @@ BYTES = 2 * (B * CS * D + D * 2 * D + D + 2 * D + HD) + 4 * 2 * B * CS * D
 
 
 def rotation_phases(nc, keep, one):
-    ratio = (1.0 + 4000.0 / 200.0) ** (1.0 / (HP - 1))
-    scale = ST * 200.0 / 1000.0
-    powers = keep.tile([P, HP], F32)
-    for j in range(8):
-        nc.vector.tensor_scalar_mul(out=powers[:, j : j + 1], in0=one[:], scalar1=ratio**j)
     partition = keep.tile([P, 1], I32)
     nc.gpsimd.iota(partition[:], pattern=[[0, 1]], base=0, channel_multiplier=1)
-    row = keep.tile([P, 1], I32)
-    nc.vector.tensor_single_scalar(out=row[:], in_=partition[:], scalar=ROWS - 1, op=ALU.bitwise_and)
-    nc.vector.tensor_scalar_mul(out=powers[:, 8:16], in0=powers[:, 0:8], scalar1=ratio**8)
-    turn_by = keep.tile([P, TOKEN_TILES], F32)
-    offset = keep.tile([P, 2, TOKEN_TILES], F32)
-    for i in range(TOKEN_TILES):
+    position = keep.tile([P, CS], I32)
+    nc.gpsimd.iota(position[:], pattern=[[1, CS]], base=0, channel_multiplier=0)
+
+    ratio = (1.0 + 4000.0 / 200.0) ** (1.0 / (HP - 1))
+    bits = keep.tile([P, 5], I32)
+    for k in range(5):
+        nc.vector.tensor_single_scalar(out=bits[:, k : k + 1], in_=partition[:], scalar=2 << k, op=ALU.bitwise_and)
+    odd = keep.tile([P, 1], I32)
+    nc.vector.tensor_single_scalar(out=odd[:], in_=partition[:], scalar=1, op=ALU.bitwise_and)
+    factors = keep.tile([P, 5], F32)
+    for k in range(5):
         nc.vector.tensor_scalar(
-            out=turn_by[:, i : i + 1], in0=row[:], scalar1=scale, scalar2=scale * ROWS * i, op0=ALU.mult, op1=ALU.add
+            out=factors[:, k : k + 1], in0=bits[:, k : k + 1], scalar1=(ratio ** (1 << k) - 1.0) / (2 << k), scalar2=1.0,
+            op0=ALU.mult, op1=ALU.add,
         )
-        for a in range(2):
-            nc.vector.tensor_scalar(
-                out=offset[:, a, i : i + 1], in0=row[:], scalar1=-scale, scalar2=a * 0.5 * PI - scale * ROWS * i,
-                op0=ALU.mult, op1=ALU.add,
-            )
-    nc.vector.tensor_scalar_mul(out=powers[:, 16:32], in0=powers[:, 0:16], scalar1=ratio**16)
-    phase = keep.tile([P, 2, TOKEN_TILES, HP], F32)
-    for a in range(2):
-        for i in range(TOKEN_TILES):
-            nc.vector.tensor_scalar(
-                out=phase[:, a, i, :], in0=powers[:], scalar1=turn_by[:, i : i + 1], scalar2=offset[:, a, i : i + 1],
-                op0=ALU.mult, op1=ALU.add,
-            )
-
-    turns = keep.tile([P, 2, TOKEN_TILES, HP], F32)
-    flat = "p a i j -> p (a i j)"
-
-    def subtract_turns(part_of_two_pi):
-        nc.vector.scalar_tensor_tensor(
-            out=phase[:].rearrange(flat), in0=turns[:].rearrange(flat), scalar=-part_of_two_pi,
-            in1=phase[:].rearrange(flat), op0=ALU.mult, op1=ALU.add,
-        )
-
-    last_steps = [
-        lambda: nc.vector.tensor_scalar(
-            out=turns[:], in0=phase[:], scalar1=1.0 / TWO_PI, scalar2=ROUND_TO_INTEGER, op0=ALU.mult, op1=ALU.add
-        ),
-        lambda: nc.vector.tensor_scalar_sub(out=turns[:], in0=turns[:], scalar1=ROUND_TO_INTEGER),
-        lambda: subtract_turns(TWO_PI_HIGH),
-        lambda: subtract_turns(TWO_PI_LOW),
-    ]
-    return phase, last_steps
-
-
-def rotation_tables(nc, keep, sin_cos, ln_gain):
-    gain_halves = ln_gain[:].rearrange("p (j e) -> p e j", e=2)
-    sin, cos = sin_cos[:, 0], sin_cos[:, 1]
-
-    same = keep.tile([P, TOKEN_TILES, 2, HP], F32)
-    cross = keep.tile([P, TOKEN_TILES, 2, HP], F32)
-    shape = [P, TOKEN_TILES, HP]
-    for e in range(2):
-        gain = gain_halves[:, e, :].unsqueeze(1).to_broadcast(shape)
-        nc.vector.tensor_tensor(out=same[:, :, e, :], in0=cos, in1=gain, op=ALU.mult)
-    nc.vector.tensor_tensor(
-        out=cross[:, :, 0, :], in0=sin, in1=gain_halves[:, 1, :].unsqueeze(1).to_broadcast(shape), op=ALU.mult
-    )
+    sign = keep.tile([P, 1], F32)
+    nc.vector.tensor_scalar(out=sign[:], in0=odd[:], scalar1=-2.0, scalar2=1.0, op0=ALU.mult, op1=ALU.add)
+    pairs = keep.tile([P, 2], F32)
+    nc.vector.tensor_tensor(out=pairs[:], in0=factors[:, 0:2], in1=factors[:, 2:4], op=ALU.mult)
+    power = keep.tile([P, 1], F32)
     nc.vector.scalar_tensor_tensor(
-        out=cross[:, :, 1, :], in0=sin, scalar=-1.0,
-        in1=gain_halves[:, 0, :].unsqueeze(1).to_broadcast(shape), op0=ALU.mult, op1=ALU.mult,
+        out=power[:], in0=pairs[:, 0:1], scalar=pairs[:, 1:2], in1=factors[:, 4:5], op0=ALU.mult, op1=ALU.mult
     )
-    return same, cross
-
-
-def inverse_rms(nc, small, sum_sq, count, width, name):
-    inverse = small.tile([P, width], F32, name="inverse_" + name)
-    nc.scalar.activation(
-        out=inverse[:], in_=sum_sq[:], func=ACT.Abs_reciprocal_sqrt, scale=1.0 / count, bias=EPS
+    turn = keep.tile([P, 1], F32)
+    nc.vector.tensor_scalar(
+        out=turn[:], in0=power[:], scalar1=1.0, scalar2=ST * 200.0 / 1000.0, op0=ALU.subtract, op1=ALU.mult
     )
-    return inverse
+    phase = keep.tile([P, 2, CS], F32)
+    for a in range(2):
+        nc.vector.tensor_scalar(
+            out=phase[:, a, :], in0=position[:], scalar1=turn[:, 0:1], scalar2=a * 0.5 * PI, op0=ALU.mult, op1=ALU.add
+        )
+
+    turns = keep.tile([P, 2, CS], F32)
+    nc.vector.tensor_scalar(
+        out=turns[:], in0=phase[:], scalar1=1.0 / TWO_PI, scalar2=ROUND_TO_INTEGER, op0=ALU.mult, op1=ALU.add
+    )
+    nc.vector.tensor_scalar_sub(out=turns[:], in0=turns[:], scalar1=ROUND_TO_INTEGER)
+    for part in (TWO_PI_HIGH, TWO_PI_LOW):
+        nc.vector.scalar_tensor_tensor(
+            out=phase[:], in0=turns[:], scalar=-part, in1=phase[:], op0=ALU.mult, op1=ALU.add
+        )
+    return phase, sign
 
 
 def tile_attention_pb_kernel(tc, x, rmskv_w, kv_w, kv_b, ln_w, out_0, out_1):
@@ -123,32 +96,39 @@ def tile_attention_pb_kernel(tc, x, rmskv_w, kv_w, kv_b, ln_w, out_0, out_1):
         tc.tile_pool(name="keep", bufs=1) as keep,
         tc.tile_pool(name="stage", bufs=4) as stage,
         tc.tile_pool(name="small", bufs=4) as small,
-        tc.psum_pool(name="flipped", bufs=4) as flipped,
-        tc.psum_pool(name="products", bufs=4) as products,
+        tc.psum_pool(name="banks", bufs=7) as banks,
+        tc.psum_pool(name="columns", bufs=1) as columns,
         tc.manual_schedule(),
     ):
+        tiles = range(TOKEN_TILES)
+        passes = range(PASSES)
+        first_values, last = KEY_CHUNKS, CHUNKS - 1
+
         x_sb = keep.tile([P, TOKEN_TILES, D], BF16)
-        x_rows = x.rearrange("b (i r s) f -> r s b i f", i=TOKEN_TILES, r=ROWS, s=ST)
+        x_rows = x.rearrange("b (r i s) f -> r s b i f", i=TOKEN_TILES, r=ROWS, s=ST)
         for r in range(ROWS):
             nc.sync.dma_start(out=x_sb[r:P:ROWS, :, :], in_=x_rows[r, 0])
 
         gain_row = keep.tile([P, D], BF16)
         nc.vector.memset(gain_row[:], 0.0)
         nc.scalar.dma_start(out=gain_row[0:1, :], in_=rmskv_w.rearrange("(o f) -> o f", o=1))
+        vector_rows = keep.tile([P, P], BF16)
+        nc.vector.memset(vector_rows[:], 0.0)
+        nc.scalar.dma_start(out=vector_rows[0:KEY_TILES, :], in_=kv_b[0:D].rearrange("(c p) -> c p", p=P))
+        for h in range(HEADS_OF_TILE):
+            nc.scalar.dma_start(
+                out=vector_rows[LN_ROW : LN_ROW + 1, h * HD : (h + 1) * HD], in_=ln_w.rearrange("(o f) -> o f", o=1)
+            )
 
-        bias = keep.tile([P, 2 * D], BF16)
+        value_bias = keep.tile([P, D], BF16)
         w_rows = kv_w.rearrange("(g p t) n -> g p t n", g=PASSES, t=PACK)
         w_raw = {}
         for n in range(CHUNKS):
-            if 0 < n <= 2:
-                half = slice((n - 1) * D, n * D)
-                nc.sync.dma_start(out=bias[:, half], in_=kv_b[half].partition_broadcast(P))
-            for g in range(PASSES):
+            if n == first_values:
+                nc.sync.dma_start(out=value_bias[:], in_=kv_b[D : 2 * D].partition_broadcast(P))
+            for g in passes:
                 w_raw[n, g] = keep.tile([P, PACK, N_TILE], BF16, name="w_raw_%d_%d" % (n, g))
                 nc.sync.dma_start(out=w_raw[n, g][:], in_=w_rows[g, :, :, n * N_TILE : (n + 1) * N_TILE])
-
-        ln_gain = keep.tile([P, HD], BF16)
-        nc.scalar.dma_start(out=ln_gain[:], in_=ln_w.partition_broadcast(P))
 
         def load_root_table():
             nc.scalar.activation(out=warm[:], in_=one[:], func=ACT.Abs_reciprocal_sqrt)
@@ -157,9 +137,21 @@ def tile_attention_pb_kernel(tc, x, rmskv_w, kv_w, kv_b, ln_w, out_0, out_1):
         nc.vector.memset(one[:], 1.0)
         warm = keep.tile([P, 1], F32)
         load_root_table()
-        phase, last_steps = rotation_phases(nc, keep, one)
+        ones = keep.tile([P, P], BF16)
+        nc.vector.memset(ones[:], 1.0)
+        phase, sign = rotation_phases(nc, keep, one)
         identity = keep.tile([P, P], F32)
         make_identity(nc, identity[:])
+        swap = keep.tile([P, P], F32)
+        for e in range(2):
+            nc.vector.tensor_copy(
+                out=swap[:].rearrange("p (j e) -> p e j", e=2)[:, e, :],
+                in_=identity[:].rearrange("p (j e) -> p e j", e=2)[:, 1 - e, :],
+            )
+        heads_of = keep.tile([P, HEADS_OF_TILE], F32)
+        nc.vector.memset(heads_of[:], 0.0)
+        for h in range(HEADS_OF_TILE):
+            nc.vector.memset(heads_of[h * HD : (h + 1) * HD, h : h + 1], 1.0)
 
         w_grouped, w_codes, w_scales = {}, {}, {}
 
@@ -178,214 +170,239 @@ def tile_attention_pb_kernel(tc, x, rmskv_w, kv_w, kv_b, ln_w, out_0, out_1):
                 in_=w_grouped[n, g][:].rearrange("p w t -> p (w t)"),
             )
 
-        x_inverse, x_turned, x_codes, x_scales = {}, {}, {}, {}
-
-        x_sum_sq = {}
+        x_sum_sq = small.tile([P, TOKEN_TILES], F32)
 
         def token_squares(i):
             squares = stage.tile([P, D], BF16)
-            x_sum_sq[i] = small.tile([P, 1], F32, name="x_sum_sq")
-            nc.scalar.activation(out=squares[:], in_=x_sb[:, i, :], func=ACT.Square, accum_out=x_sum_sq[i][:])
+            nc.scalar.activation(
+                out=squares[:], in_=x_sb[:, i, :], func=ACT.Square, accum_out=x_sum_sq[:, i : i + 1]
+            )
 
-        def token_norm(i):
-            x_inverse[i] = inverse_rms(nc, small, x_sum_sq[i], D, 1, "x")
+        def inverse_rms(out, sum_sq, count):
+            nc.scalar.activation(out=out, in_=sum_sq, func=ACT.Abs_reciprocal_sqrt, scale=1.0 / count, bias=EPS)
 
-        ones = keep.tile([P, P], BF16)
-        nc.vector.memset(ones[:], 1.0)
         gain_all = {}
-        for g in range(PASSES):
-            gain_all[g] = products.tile([P, K_PASS], F32, name="product")
+        for g in passes:
+            gain_all[g] = banks.tile([P, K_PASS], F32, name="bank")
             nc.tensor.matmul(
                 out=gain_all[g][:], lhsT=ones[:], rhs=gain_row[:, g * K_PASS : (g + 1) * K_PASS], start=True, stop=True
             )
+        vector_columns = columns.tile([P, P], BF16, name="columns")
+        identity_bf16 = keep.tile([P, P], BF16)
+        nc.vector.tensor_copy(out=identity_bf16[:], in_=identity[:])
+        nc.tensor.transpose(vector_columns[:], vector_rows[:], identity_bf16[:])
 
-        x_normed, x_grouped = {}, {}
+        x_normed, x_turned, x_grouped, x_codes, x_scales = {}, {}, {}, {}, {}
 
-        def norm_tokens(i, short_steps):
-            x_normed[i] = stage.tile([P, D], BF16, name="x_normed")
-            for g in range(PASSES):
-                features = slice(g * K_PASS, (g + 1) * K_PASS)
-                nc.vector.scalar_tensor_tensor(
-                    out=x_normed[i][:, features], in0=x_sb[:, i, features], scalar=x_inverse[i][:, 0:1],
-                    in1=gain_all[g][:], op0=ALU.mult, op1=ALU.mult,
-                )
-                for step in short_steps[g : g + 1]:
-                    step()
-
-        def turn_tokens(i):
-            words = x_normed[i][:].bitcast(F32)
-            words_of_pass = K_PASS // 2
-            x_turned[i] = flipped.tile([P, PASSES, 2, P], F32, name="turned")
-            for g in range(PASSES):
-                for u in range(2):
-                    nc.tensor.transpose(
-                        x_turned[i][:, g, u, :], words[:, g * words_of_pass + u : (g + 1) * words_of_pass : 2], identity[:]
-                    )
-
-        def gather_tokens(i):
-            x_grouped[i] = stage.tile([P, PASSES, P, PACK], BF16, name="x_grouped", align_bytes=64)
-            nc.scalar.copy(out=x_grouped[i][:].bitcast(F32), in_=x_turned[i][:].rearrange("p g u r -> p g r u"))
-
-        def quantise_tokens(i):
-            x_codes[i] = keep.tile([P, PASSES * P], U32, name="x_codes_%d" % i, align_bytes=64)
-            x_scales[i] = keep.tile([P, PASSES * P], U8, name="x_scales_%d" % i, align_bytes=64)
-            nc.vector.quantize_mx(
-                out=x_codes[i][:].bitcast(FP8X4), scales=x_scales[i][:],
-                in_=x_grouped[i][:].rearrange("p g r t -> p (g r t)"),
+        def norm_tokens(i, g):
+            x_normed[i, g] = stage.tile([P, K_PASS], BF16, name="x_normed")
+            nc.vector.scalar_tensor_tensor(
+                out=x_normed[i, g][:], in0=x_sb[:, i, g * K_PASS : (g + 1) * K_PASS], scalar=x_inverse[:, i : i + 1],
+                in1=gain_all[g][:], op0=ALU.mult, op1=ALU.mult,
             )
 
+        def turn_tokens(g):
+            x_turned[g] = banks.tile([P, TOKEN_TILES, 2, P], F32, name="bank")
+            for i in tiles:
+                for u in range(2):
+                    nc.tensor.transpose(x_turned[g][:, i, u, :], x_normed[i, g][:].bitcast(F32)[:, u::2], identity[:])
+
+        def gather_tokens(g):
+            x_grouped[g] = stage.tile([P, TOKEN_TILES, P, PACK], BF16, name="x_grouped", align_bytes=64)
+            nc.scalar.copy(out=x_grouped[g][:].bitcast(F32), in_=x_turned[g][:].rearrange("p i u r -> p i r u"))
+
+        def quantise_tokens(g):
+            x_codes[g] = keep.tile([P, TOKENS], U32, name="x_codes_%d" % g, align_bytes=64)
+            x_scales[g] = keep.tile([P, TOKENS], U8, name="x_scales_%d" % g, align_bytes=64)
+            nc.vector.quantize_mx(
+                out=x_codes[g][:].bitcast(FP8X4), scales=x_scales[g][:],
+                in_=x_grouped[g][:].rearrange("p i r t -> p (i r t)"),
+            )
+
+        key_products, key_squares, key_sums, key_inverse, own, partner, rotated = {}, {}, {}, {}, {}, {}, {}
+
+        def multiply_keys(n):
+            for b in range(TILES_OF_CHUNK // 2):
+                key_products[n, b] = banks.tile([P, 2, TOKENS], F32, name="bank")
+                for k in range(2):
+                    channels = slice((2 * b + k) * P, (2 * b + k + 1) * P)
+                    for g in passes:
+                        nc.tensor.matmul_mx(
+                            out=key_products[n, b][:, k, :],
+                            lhsT=w_codes[n, g][:, channels].bitcast(FP8X4), lhsT_scale=w_scales[n, g][:, channels],
+                            rhs=x_codes[g][:].bitcast(FP8X4), rhs_scale=x_scales[g][:],
+                            start=(g == 0), stop=(g == PASSES - 1),
+                        )
+
+        def square_keys(n, b):
+            for k in range(2):
+                c = 2 * b + k
+                nc.scalar.activation(
+                    out=key_squares[n][:, c, :], in_=key_products[n, b][:, k, :], func=ACT.Square,
+                    bias=key_bias[:, n * TILES_OF_CHUNK + c : n * TILES_OF_CHUNK + c + 1],
+                )
+
+        def weigh_keys(n, b):
+            for k in range(2):
+                c = 2 * b + k
+                for weighed, factor in ((own, own_factor), (partner, partner_factor)):
+                    nc.vector.scalar_tensor_tensor(
+                        out=weighed[n][:, c, :], in0=key_products[n, b][:, k, :],
+                        scalar=key_bias[:, n * TILES_OF_CHUNK + c : n * TILES_OF_CHUNK + c + 1],
+                        in1=factor[:], op0=ALU.add, op1=ALU.mult,
+                    )
+
+        def weigh_chunk(n):
+            key_squares[n] = stage.tile([P, TILES_OF_CHUNK, TOKENS], F32, name="key_squares")
+            own[n] = stage.tile([P, TILES_OF_CHUNK, TOKENS], F32, name="own")
+            partner[n] = stage.tile([P, TILES_OF_CHUNK, TOKENS], F32, name="partner")
+            for b in range(TILES_OF_CHUNK // 2):
+                weigh_keys(n, b)
+                square_keys(n, b)
+
+        def turn_keys(n):
+            for i in tiles:
+                rotated[n, i] = banks.tile([P, TILES_OF_CHUNK, P], F32, name="bank")
+            for c in range(TILES_OF_CHUNK):
+                for i in tiles:
+                    tokens = slice(i * P, (i + 1) * P)
+                    nc.tensor.matmul(
+                        out=rotated[n, i][:, c, :], lhsT=own[n][:, c, tokens], rhs=identity[:],
+                        is_transpose=True, start=True, stop=False,
+                    )
+                    nc.tensor.matmul(
+                        out=rotated[n, i][:, c, :], lhsT=partner[n][:, c, tokens], rhs=swap[:],
+                        is_transpose=True, start=False, stop=True,
+                    )
+
+        def sum_squares(n):
+            key_sums[n] = columns.tile([P, TOKEN_TILES, HEADS], F32, name="columns")
+            for c in range(TILES_OF_CHUNK):
+                for i in tiles:
+                    nc.tensor.matmul(
+                        out=key_sums[n][:, i, c * HEADS_OF_TILE : (c + 1) * HEADS_OF_TILE],
+                        lhsT=key_squares[n][:, c, i * P : (i + 1) * P], rhs=heads_of[:], start=True, stop=True,
+                    )
+
+        def key_root(n):
+            key_inverse[n] = small.tile([P, TOKEN_TILES, HEADS], F32, name="key_inverse")
+            inverse_rms(key_inverse[n][:], key_sums[n][:], HD)
+
+        results = {}
+
+        def store(out, first_head, result):
+            for r in range(ROWS):
+                nc.sync.dma_start(
+                    out=out[:, first_head : first_head + HEADS, TOKEN_TILES * r : TOKEN_TILES * (r + 1), :].rearrange(
+                        "b h i d -> b h (i d)"
+                    ),
+                    in_=result[r:P:ROWS, :, :, :].rearrange("p h i d -> p h (i d)"),
+                )
+
+        def normalise_keys(n, i):
+            if i == 0:
+                results[n] = stage.tile([P, HEADS, TOKEN_TILES, HD], F32, name="key_result")
+            nc.vector.tensor_tensor(
+                out=results[n][:, :, i, :], in0=rotated[n, i][:].rearrange("p c (h d) -> p (c h) d", d=HD),
+                in1=key_inverse[n][:, i, :].unsqueeze(2).to_broadcast([P, HEADS, HD]), op=ALU.mult,
+            )
+            if i == TOKEN_TILES - 1:
+                store(out_0, n * HEADS, results[n])
+
         def multiply_pass(n, i, g, product):
-            tokens = slice(g * P, (g + 1) * P)
+            tokens = slice(i * P, (i + 1) * P)
             nc.tensor.matmul_mx(
                 out=product[:],
-                lhsT=x_codes[i][:, tokens].bitcast(FP8X4), lhsT_scale=x_scales[i][:, tokens],
+                lhsT=x_codes[g][:, tokens].bitcast(FP8X4), lhsT_scale=x_scales[g][:, tokens],
                 rhs=w_codes[n, g][:].bitcast(FP8X4), rhs_scale=w_scales[n, g][:],
                 start=(g == 0), stop=(g == PASSES - 1),
             )
 
-        def multiply(n, i):
-            product = products.tile([P, N_TILE], F32, name="product")
-            for g in range(PASSES):
-                multiply_pass(n, i, g, product)
-            return product
-
-        def store(out, first_head, i, result, queues=(nc.sync,)):
-            for r in range(ROWS):
-                queues[r % len(queues)].dma_start(
-                    out=out[:, first_head : first_head + HEADS, ROWS * i + r, :], in_=result[r:P:ROWS, :, :]
-                )
-
-        def values(n, i, product, queues=(nc.sync,)):
-            result = stage.tile([P, HEADS, HD], F32, name="value_result")
+        def values(n, i, product):
+            if i == 0:
+                results[n] = stage.tile([P, HEADS, TOKEN_TILES, HD], F32, name="value_result")
+            columns_of_chunk = slice((n - KEY_CHUNKS) * N_TILE, (n - KEY_CHUNKS + 1) * N_TILE)
             nc.vector.tensor_tensor(
-                out=result[:].rearrange("p h d -> p (h d)"), in0=product[:],
-                in1=bias[:, n * N_TILE : (n + 1) * N_TILE], op=ALU.add,
+                out=results[n][:, :, i, :], in0=product[:].rearrange("p (h d) -> p h d", d=HD),
+                in1=value_bias[:, columns_of_chunk].rearrange("p (h d) -> p h d", d=HD), op=ALU.add,
             )
-            store(out_1, (n - KEY_CHUNKS) * HEADS, i, result, queues)
+            if i == TOKEN_TILES - 1:
+                store(out_1, (n - KEY_CHUNKS) * HEADS, results[n])
 
-        keys, key_sum_sq, key_inverse, by_same, by_cross, rotated = {}, {}, {}, {}, {}, {}
-        every_head = [P, HEADS, 2, HP]
-
-        def biased_keys(n, i):
-            product = multiply(n, i)
-            halves = "p (h j e) -> p h e j"
-            keys[i] = stage.tile([P, HEADS, 2, HP], F32, name="keys")
-            nc.vector.tensor_tensor(
-                out=keys[i][:], in0=product[:].rearrange(halves, e=2, j=HP),
-                in1=bias[:, n * N_TILE : (n + 1) * N_TILE].rearrange(halves, e=2, j=HP), op=ALU.add,
-            )
-
-        def key_norm(n, i):
-            key_squares = stage.tile([P, HEADS, HD], F32)
-            key_sum_sq[i] = small.tile([P, HEADS], F32, name="key_sum_sq")
-            for h in range(HEADS):
-                nc.scalar.activation(
-                    out=key_squares[:, h, :], in_=keys[i][:, h].rearrange("p e j -> p (e j)"), func=ACT.Square,
-                    accum_out=key_sum_sq[i][:, h : h + 1],
-                )
-
-        def key_root(n, i):
-            key_inverse[n, i] = inverse_rms(nc, small, key_sum_sq[i], HD, HEADS, "k")
-
-        def times_same(i):
-            by_same[i] = stage.tile(every_head, F32, name="by_same")
-            nc.vector.tensor_tensor(
-                out=by_same[i][:], in0=keys[i][:], in1=same[:, i].unsqueeze(1).to_broadcast(every_head), op=ALU.mult
-            )
-
-        def times_cross(i):
-            by_cross[i] = stage.tile(every_head, F32, name="by_cross")
-            nc.vector.tensor_tensor(
-                out=by_cross[i][:], in0=keys[i][:], in1=cross[:, i].unsqueeze(1).to_broadcast(every_head), op=ALU.mult
-            )
-
-        def add_halves(n, i):
-            rotated[n, i] = stage.tile(every_head, F32, name="rotated")
-            for e in range(2):
-                nc.vector.tensor_tensor(
-                    out=rotated[n, i][:, :, e, :], in0=by_same[i][:, :, e, :], in1=by_cross[i][:, :, 1 - e, :], op=ALU.add
-                )
-
-        def normalise_keys(n, i):
-            result = stage.tile([P, HEADS, HD], F32, name="key_result")
-            nc.vector.tensor_tensor(
-                out=result[:].rearrange("p h (j e) -> p h j e", e=2),
-                in0=rotated[n, i][:].rearrange("p h e j -> p h j e"),
-                in1=key_inverse[n, i][:].unsqueeze(2).unsqueeze(3).to_broadcast([P, HEADS, HP, 2]), op=ALU.mult,
-            )
-            store(out_0, n * HEADS, i, result)
-
-        for i in range(TOKEN_TILES):
+        for i in tiles:
             token_squares(i)
-        for i in range(TOKEN_TILES):
-            token_norm(i)
+        x_inverse = small.tile([P, TOKEN_TILES], F32)
+        inverse_rms(x_inverse[:], x_sum_sq[:], D)
         regroup(nc.vector.tensor_copy, 0, 0)
-        last_steps[0]()
-        for i in range(TOKEN_TILES):
-            norm_tokens(i, last_steps[1 + 2 * i :  3 + 2 * i])
-            turn_tokens(i)
-        sin_cos = keep.tile([P, 2, TOKEN_TILES, HP], F32)
+        for g in passes:
+            for i in tiles:
+                norm_tokens(i, g)
+            turn_tokens(g)
+        sin_cos = keep.tile([P, 2, CS], F32)
         nc.scalar.activation(out=sin_cos[:], in_=phase[:], func=ACT.Sin)
-        for i in range(TOKEN_TILES):
-            gather_tokens(i)
+        for g in passes:
+            gather_tokens(g)
         load_root_table()
+        key_bias = keep.tile([P, KEY_TILES], F32)
+        nc.vector.tensor_copy(out=key_bias[:], in_=vector_columns[:, 0:KEY_TILES])
+        own_gain = keep.tile([P, 1], F32)
+        nc.vector.tensor_copy(out=own_gain[:], in_=vector_columns[:, LN_ROW : LN_ROW + 1])
+        partner_column = columns.tile([P, 1], F32, name="columns")
+        nc.tensor.matmul(out=partner_column[:], lhsT=swap[:], rhs=own_gain[:], start=True, stop=True)
         regroup(nc.vector.tensor_copy, 0, 1)
         quantise(0, 0)
         quantise_tokens(0)
         quantise(0, 1)
         quantise_tokens(1)
-        regroup(nc.vector.tensor_copy, 1, 0)
-        same, cross = rotation_tables(nc, keep, sin_cos, ln_gain)
+        multiply_keys(0)
         regroup(nc.scalar.copy, 1, 1)
+        partner_gain = keep.tile([P, 1], F32)
+        nc.vector.tensor_tensor(out=partner_gain[:], in0=partner_column[:], in1=sign[:], op=ALU.mult)
+        regroup(nc.vector.tensor_copy, 1, 0)
+        own_factor = keep.tile([P, TOKENS], F32)
+        partner_factor = keep.tile([P, TOKENS], F32)
+        for factor, table, gain in ((own_factor, 1, own_gain), (partner_factor, 0, partner_gain)):
+            nc.vector.tensor_scalar_mul(
+                out=factor[:].rearrange("p (i b r) -> p i b r", i=TOKEN_TILES, r=ROWS),
+                in0=sin_cos[:, table, :].rearrange("p (r i) -> p i r", r=ROWS).unsqueeze(2).to_broadcast(
+                    [P, TOKEN_TILES, B, ROWS]
+                ),
+                scalar1=gain[:, 0:1],
+            )
 
-        tiles = range(TOKEN_TILES)
-        passes = range(PASSES)
-        first_values, last = KEY_CHUNKS, CHUNKS - 1
-        for i in tiles:
-            biased_keys(0, i)
-        for i in tiles:
-            key_norm(0, i)
-        for i in tiles:
-            key_root(0, i)
-        for g in passes:
-            regroup(nc.scalar.copy, first_values, g)
-        for i in tiles:
-            times_same(i)
+        weigh_chunk(0)
+        turn_keys(0)
+        regroup(nc.scalar.copy, first_values, 1)
         for g in passes:
             quantise(1, g)
-        for i in tiles:
-            times_cross(i)
-        for i in tiles:
-            add_halves(0, i)
-        for i in tiles:
-            normalise_keys(0, i)
-        for i in tiles:
-            biased_keys(1, i)
-        for i in tiles:
-            key_norm(1, i)
-        for i in tiles:
-            key_root(1, i)
-        for g in passes:
-            regroup(nc.scalar.copy, last, g)
+        multiply_keys(1)
+        sum_squares(0)
+        regroup(nc.vector.tensor_copy, first_values, 0)
+        regroup(nc.scalar.copy, last, 0)
+        weigh_chunk(1)
+        turn_keys(1)
+        key_root(0)
+        regroup(nc.scalar.copy, last, 1)
         for g in passes:
             quantise(first_values, g)
-        value_products = [multiply(first_values, i) for i in tiles]
         for i in tiles:
-            times_same(i)
+            normalise_keys(0, i)
+        value_products = [banks.tile([P, N_TILE], F32, name="bank") for i in tiles]
         for i in tiles:
-            times_cross(i)
-        for i in tiles:
-            values(first_values, i, value_products[i])
-        for i in tiles:
-            add_halves(1, i)
-        last_products = [products.tile([P, N_TILE], F32, name="product") for i in tiles]
+            for g in passes:
+                multiply_pass(first_values, i, g, value_products[i])
+        sum_squares(1)
+        key_root(1)
         quantise(last, 0)
+        last_products = [banks.tile([P, N_TILE], F32, name="bank") for i in tiles]
         for i in tiles:
             multiply_pass(last, i, 0, last_products[i])
         for i in tiles:
-            normalise_keys(1, i)
+            values(first_values, i, value_products[i])
         quantise(last, 1)
         for i in tiles:
             multiply_pass(last, i, 1, last_products[i])
+        for i in tiles:
+            normalise_keys(1, i)
         for i in tiles:
             values(last, i, last_products[i])

@@ -30,7 +30,6 @@ HEADS = N_TILE // HD
 KEY_TILES = D // P
 TILES_OF_CHUNK = N_TILE // P
 HEADS_OF_TILE = P // HD
-LN_ROW = 32
 
 PI = 3.141592653589793
 TWO_PI = 2.0 * PI
@@ -105,38 +104,35 @@ def tile_attention_pb_kernel(tc, x, rmskv_w, kv_w, kv_b, ln_w, out_0, out_1):
         first_values, last = KEY_CHUNKS, CHUNKS - 1
 
         x_sb = keep.tile([P, TOKEN_TILES, D], BF16)
-        x_rows = x.rearrange("b (r i s) f -> r s b i f", i=TOKEN_TILES, r=ROWS, s=ST)
-        for r in range(ROWS):
-            nc.sync.dma_start(out=x_sb[r:P:ROWS, :, :], in_=x_rows[r, 0])
+        x_rows = x.rearrange("b t f -> (b t) f").rearrange("(p i s) f -> i s p f", i=TOKEN_TILES, s=ST)
+        for i in tiles:
+            nc.sync.dma_start(out=x_sb[:, i, :], in_=x_rows[i, 0])
+
+        def load_root_table():
+            nc.scalar.activation(out=warm[:], in_=one[:], func=ACT.Abs_reciprocal_sqrt)
 
         gain_row = keep.tile([P, D], BF16)
-        nc.vector.memset(gain_row[:], 0.0)
-        nc.scalar.dma_start(out=gain_row[0:1, :], in_=rmskv_w.rearrange("(o f) -> o f", o=1))
+        nc.vector.memset(gain_row[:].bitcast(I32), 0)
+        nc.sync.dma_start(out=gain_row[0:1, :], in_=rmskv_w.rearrange("(o f) -> o f", o=1))
+        one = keep.tile([P, 1], F32)
+        nc.vector.memset(one[:], 1.0)
+        warm = keep.tile([P, 1], F32)
+        load_root_table()
         vector_rows = keep.tile([P, P], BF16)
-        nc.vector.memset(vector_rows[:], 0.0)
+        nc.vector.memset(vector_rows[:].bitcast(I32), 0)
         nc.scalar.dma_start(out=vector_rows[0:KEY_TILES, :], in_=kv_b[0:D].rearrange("(c p) -> c p", p=P))
-        for h in range(HEADS_OF_TILE):
-            nc.scalar.dma_start(
-                out=vector_rows[LN_ROW : LN_ROW + 1, h * HD : (h + 1) * HD], in_=ln_w.rearrange("(o f) -> o f", o=1)
-            )
+        ln_gain = keep.tile([P, HD], BF16)
+        nc.scalar.dma_start(out=ln_gain[:], in_=ln_w.partition_broadcast(P))
 
         value_bias = keep.tile([P, D], BF16)
         w_rows = kv_w.rearrange("(g p t) n -> g p t n", g=PASSES, t=PACK)
         w_raw = {}
         for n in range(CHUNKS):
-            if n == first_values:
-                nc.sync.dma_start(out=value_bias[:], in_=kv_b[D : 2 * D].partition_broadcast(P))
             for g in passes:
                 w_raw[n, g] = keep.tile([P, PACK, N_TILE], BF16, name="w_raw_%d_%d" % (n, g))
                 nc.sync.dma_start(out=w_raw[n, g][:], in_=w_rows[g, :, :, n * N_TILE : (n + 1) * N_TILE])
+        nc.sync.dma_start(out=value_bias[:], in_=kv_b[D : 2 * D].partition_broadcast(P))
 
-        def load_root_table():
-            nc.scalar.activation(out=warm[:], in_=one[:], func=ACT.Abs_reciprocal_sqrt)
-
-        one = keep.tile([P, 1], F32)
-        nc.vector.memset(one[:], 1.0)
-        warm = keep.tile([P, 1], F32)
-        load_root_table()
         ones = keep.tile([P, P], BF16)
         nc.vector.memset(ones[:], 1.0)
         phase, sign = rotation_phases(nc, keep, one)
@@ -148,10 +144,6 @@ def tile_attention_pb_kernel(tc, x, rmskv_w, kv_w, kv_b, ln_w, out_0, out_1):
                 out=swap[:].rearrange("p (j e) -> p e j", e=2)[:, e, :],
                 in_=identity[:].rearrange("p (j e) -> p e j", e=2)[:, 1 - e, :],
             )
-        heads_of = keep.tile([P, HEADS_OF_TILE], F32)
-        nc.vector.memset(heads_of[:], 0.0)
-        for h in range(HEADS_OF_TILE):
-            nc.vector.memset(heads_of[h * HD : (h + 1) * HD, h : h + 1], 1.0)
 
         w_grouped, w_codes, w_scales = {}, {}, {}
 
@@ -187,10 +179,8 @@ def tile_attention_pb_kernel(tc, x, rmskv_w, kv_w, kv_b, ln_w, out_0, out_1):
             nc.tensor.matmul(
                 out=gain_all[g][:], lhsT=ones[:], rhs=gain_row[:, g * K_PASS : (g + 1) * K_PASS], start=True, stop=True
             )
-        vector_columns = columns.tile([P, P], BF16, name="columns")
         identity_bf16 = keep.tile([P, P], BF16)
         nc.vector.tensor_copy(out=identity_bf16[:], in_=identity[:])
-        nc.tensor.transpose(vector_columns[:], vector_rows[:], identity_bf16[:])
 
         x_normed, x_turned, x_grouped, x_codes, x_scales = {}, {}, {}, {}, {}
 
@@ -219,7 +209,7 @@ def tile_attention_pb_kernel(tc, x, rmskv_w, kv_w, kv_b, ln_w, out_0, out_1):
                 in_=x_grouped[g][:].rearrange("p i r t -> p (i r t)"),
             )
 
-        key_products, key_squares, key_sums, key_inverse, own, partner, rotated = {}, {}, {}, {}, {}, {}, {}
+        key_products, key_sums, key_inverse, own, partner, rotated = {}, {}, {}, {}, {}, {}
 
         def multiply_keys(n):
             for b in range(TILES_OF_CHUNK // 2):
@@ -234,14 +224,6 @@ def tile_attention_pb_kernel(tc, x, rmskv_w, kv_w, kv_b, ln_w, out_0, out_1):
                             start=(g == 0), stop=(g == PASSES - 1),
                         )
 
-        def square_keys(n, b):
-            for k in range(2):
-                c = 2 * b + k
-                nc.scalar.activation(
-                    out=key_squares[n][:, c, :], in_=key_products[n, b][:, k, :], func=ACT.Square,
-                    bias=key_bias[:, n * TILES_OF_CHUNK + c : n * TILES_OF_CHUNK + c + 1],
-                )
-
         def weigh_keys(n, b):
             for k in range(2):
                 c = 2 * b + k
@@ -253,12 +235,10 @@ def tile_attention_pb_kernel(tc, x, rmskv_w, kv_w, kv_b, ln_w, out_0, out_1):
                     )
 
         def weigh_chunk(n):
-            key_squares[n] = stage.tile([P, TILES_OF_CHUNK, TOKENS], F32, name="key_squares")
             own[n] = stage.tile([P, TILES_OF_CHUNK, TOKENS], F32, name="own")
             partner[n] = stage.tile([P, TILES_OF_CHUNK, TOKENS], F32, name="partner")
             for b in range(TILES_OF_CHUNK // 2):
                 weigh_keys(n, b)
-                square_keys(n, b)
 
         def turn_keys(n):
             for i in tiles:
@@ -275,13 +255,16 @@ def tile_attention_pb_kernel(tc, x, rmskv_w, kv_w, kv_b, ln_w, out_0, out_1):
                         is_transpose=True, start=False, stop=True,
                     )
 
+        def head(n, i, h):
+            return rotated[n, i][:, h // HEADS_OF_TILE, (h % HEADS_OF_TILE) * HD : (h % HEADS_OF_TILE + 1) * HD]
+
         def sum_squares(n):
-            key_sums[n] = columns.tile([P, TOKEN_TILES, HEADS], F32, name="columns")
-            for c in range(TILES_OF_CHUNK):
-                for i in tiles:
-                    nc.tensor.matmul(
-                        out=key_sums[n][:, i, c * HEADS_OF_TILE : (c + 1) * HEADS_OF_TILE],
-                        lhsT=key_squares[n][:, c, i * P : (i + 1) * P], rhs=heads_of[:], start=True, stop=True,
+            squares = stage.tile([P, HEADS, HD], F32, name="head_squares")
+            key_sums[n] = small.tile([P, TOKEN_TILES, HEADS], F32, name="key_sums")
+            for i in tiles:
+                for h in range(HEADS):
+                    nc.scalar.activation(
+                        out=squares[:, h, :], in_=head(n, i, h), func=ACT.Square, accum_out=key_sums[n][:, i, h : h + 1]
                     )
 
         def key_root(n):
@@ -302,10 +285,11 @@ def tile_attention_pb_kernel(tc, x, rmskv_w, kv_w, kv_b, ln_w, out_0, out_1):
         def normalise_keys(n, i):
             if i == 0:
                 results[n] = stage.tile([P, HEADS, TOKEN_TILES, HD], F32, name="key_result")
-            nc.vector.tensor_tensor(
-                out=results[n][:, :, i, :], in0=rotated[n, i][:].rearrange("p c (h d) -> p (c h) d", d=HD),
-                in1=key_inverse[n][:, i, :].unsqueeze(2).to_broadcast([P, HEADS, HD]), op=ALU.mult,
-            )
+            for h in range(HEADS):
+                nc.vector.scalar_tensor_tensor(
+                    out=results[n][:, h, i, :], in0=head(n, i, h), scalar=key_inverse[n][:, i, h : h + 1], in1=ln_gain[:],
+                    op0=ALU.mult, op1=ALU.mult,
+                )
             if i == TOKEN_TILES - 1:
                 store(out_0, n * HEADS, results[n])
 
@@ -343,46 +327,44 @@ def tile_attention_pb_kernel(tc, x, rmskv_w, kv_w, kv_b, ln_w, out_0, out_1):
         for g in passes:
             gather_tokens(g)
         load_root_table()
-        key_bias = keep.tile([P, KEY_TILES], F32)
-        nc.vector.tensor_copy(out=key_bias[:], in_=vector_columns[:, 0:KEY_TILES])
-        own_gain = keep.tile([P, 1], F32)
-        nc.vector.tensor_copy(out=own_gain[:], in_=vector_columns[:, LN_ROW : LN_ROW + 1])
-        partner_column = columns.tile([P, 1], F32, name="columns")
-        nc.tensor.matmul(out=partner_column[:], lhsT=swap[:], rhs=own_gain[:], start=True, stop=True)
+        vector_columns = columns.tile([P, P], BF16, name="columns")
+        nc.tensor.transpose(vector_columns[:], vector_rows[:], identity_bf16[:])
         regroup(nc.vector.tensor_copy, 0, 1)
         quantise(0, 0)
         quantise_tokens(0)
         quantise(0, 1)
         quantise_tokens(1)
+        key_bias = keep.tile([P, KEY_TILES], F32)
+        nc.vector.tensor_copy(out=key_bias[:], in_=vector_columns[:, 0:KEY_TILES])
         multiply_keys(0)
         regroup(nc.scalar.copy, 1, 1)
-        partner_gain = keep.tile([P, 1], F32)
-        nc.vector.tensor_tensor(out=partner_gain[:], in0=partner_column[:], in1=sign[:], op=ALU.mult)
         regroup(nc.vector.tensor_copy, 1, 0)
         own_factor = keep.tile([P, TOKENS], F32)
         partner_factor = keep.tile([P, TOKENS], F32)
-        for factor, table, gain in ((own_factor, 1, own_gain), (partner_factor, 0, partner_gain)):
+        for factor, table, by in ((own_factor, 1, 1.0), (partner_factor, 0, sign[:, 0:1])):
             nc.vector.tensor_scalar_mul(
                 out=factor[:].rearrange("p (i b r) -> p i b r", i=TOKEN_TILES, r=ROWS),
                 in0=sin_cos[:, table, :].rearrange("p (r i) -> p i r", r=ROWS).unsqueeze(2).to_broadcast(
                     [P, TOKEN_TILES, B, ROWS]
                 ),
-                scalar1=gain[:, 0:1],
+                scalar1=by,
             )
 
         weigh_chunk(0)
         turn_keys(0)
         regroup(nc.scalar.copy, first_values, 1)
+        sum_squares(0)
+        key_root(0)
         for g in passes:
             quantise(1, g)
         multiply_keys(1)
-        sum_squares(0)
         regroup(nc.vector.tensor_copy, first_values, 0)
         regroup(nc.scalar.copy, last, 0)
         weigh_chunk(1)
         turn_keys(1)
-        key_root(0)
         regroup(nc.scalar.copy, last, 1)
+        sum_squares(1)
+        key_root(1)
         for g in passes:
             quantise(first_values, g)
         for i in tiles:
@@ -391,8 +373,6 @@ def tile_attention_pb_kernel(tc, x, rmskv_w, kv_w, kv_b, ln_w, out_0, out_1):
         for i in tiles:
             for g in passes:
                 multiply_pass(first_values, i, g, value_products[i])
-        sum_squares(1)
-        key_root(1)
         quantise(last, 0)
         last_products = [banks.tile([P, N_TILE], F32, name="bank") for i in tiles]
         for i in tiles:

@@ -95,8 +95,7 @@ def tile_attention_pb_kernel(tc, x, rmskv_w, kv_w, kv_b, ln_w, out_0, out_1):
         tc.tile_pool(name="keep", bufs=1) as keep,
         tc.tile_pool(name="stage", bufs=4) as stage,
         tc.tile_pool(name="small", bufs=4) as small,
-        tc.psum_pool(name="banks", bufs=7) as banks,
-        tc.psum_pool(name="columns", bufs=1) as columns,
+        tc.psum_pool(name="banks", bufs=8) as banks,
         tc.manual_schedule(),
     ):
         tiles = range(TOKEN_TILES)
@@ -153,6 +152,20 @@ def tile_attention_pb_kernel(tc, x, rmskv_w, kv_w, kv_b, ln_w, out_0, out_1):
                 out=w_grouped[n, g][:].rearrange("p (c i) t -> p c t i", i=4),
                 in_=w_raw[n, g][:].rearrange("p t (c i) -> p c t i", i=4),
             )
+
+        def regroup_on_gpsimd(n, g, factor=1.0):
+            w_grouped[n, g] = stage.tile([P, N_TILE, PACK], BF16, name="w_grouped", align_bytes=64)
+            for half in range(2):
+                cols = slice(half * N_TILE // 2, (half + 1) * N_TILE // 2)
+                nc.gpsimd.tensor_scalar(
+                    out=w_grouped[n, g][:, cols, :], in0=w_raw[n, g][:, :, cols].rearrange("p t c -> p c t"),
+                    scalar1=factor, scalar2=0.0, op0=ALU.mult, op1=ALU.add,
+                )
+
+        def gate():
+            column = small.tile([P, 1], F32, name="gate")
+            nc.vector.memset(column[:], 1.0)
+            return column[:, 0:1]
 
         def quantise(n, g):
             w_codes[n, g] = keep.tile([P, N_TILE], U32, name="w_codes_%d_%d" % (n, g), align_bytes=64)
@@ -327,9 +340,9 @@ def tile_attention_pb_kernel(tc, x, rmskv_w, kv_w, kv_b, ln_w, out_0, out_1):
         for g in passes:
             gather_tokens(g)
         load_root_table()
-        vector_columns = columns.tile([P, P], BF16, name="columns")
+        vector_columns = banks.tile([P, P], BF16, name="bank")
         nc.tensor.transpose(vector_columns[:], vector_rows[:], identity_bf16[:])
-        regroup(nc.vector.tensor_copy, 0, 1)
+        regroup_on_gpsimd(0, 1)
         quantise(0, 0)
         quantise_tokens(0)
         quantise(0, 1)
@@ -350,38 +363,37 @@ def tile_attention_pb_kernel(tc, x, rmskv_w, kv_w, kv_b, ln_w, out_0, out_1):
                 scalar1=by,
             )
 
+        regroup_on_gpsimd(first_values, 1, gate())
         weigh_chunk(0)
         turn_keys(0)
-        regroup(nc.scalar.copy, first_values, 1)
+        regroup(nc.scalar.copy, first_values, 0)
         sum_squares(0)
         key_root(0)
         for g in passes:
             quantise(1, g)
         multiply_keys(1)
-        regroup(nc.vector.tensor_copy, first_values, 0)
-        regroup(nc.scalar.copy, last, 0)
-        weigh_chunk(1)
-        turn_keys(1)
-        regroup(nc.scalar.copy, last, 1)
-        sum_squares(1)
-        key_root(1)
         for g in passes:
             quantise(first_values, g)
-        for i in tiles:
-            normalise_keys(0, i)
         value_products = [banks.tile([P, N_TILE], F32, name="bank") for i in tiles]
         for i in tiles:
             for g in passes:
                 multiply_pass(first_values, i, g, value_products[i])
-        quantise(last, 0)
-        last_products = [banks.tile([P, N_TILE], F32, name="bank") for i in tiles]
+        regroup(nc.scalar.copy, last, 1)
+        regroup_on_gpsimd(last, 0, gate())
+        weigh_chunk(1)
+        turn_keys(1)
+        sum_squares(1)
+        key_root(1)
         for i in tiles:
-            multiply_pass(last, i, 0, last_products[i])
+            normalise_keys(0, i)
         for i in tiles:
             values(first_values, i, value_products[i])
-        quantise(last, 1)
+        for g in passes:
+            quantise(last, g)
+        last_products = [banks.tile([P, N_TILE], F32, name="bank") for i in tiles]
         for i in tiles:
-            multiply_pass(last, i, 1, last_products[i])
+            for g in passes:
+                multiply_pass(last, i, g, last_products[i])
         for i in tiles:
             normalise_keys(1, i)
         for i in tiles:

@@ -256,17 +256,18 @@ def tile_attention_pb_kernel(tc, x, rmskv_w, kv_w, kv_b, ln_w, out_0, out_1):
         def turn_keys(n):
             for i in tiles:
                 rotated[n, i] = banks.tile([P, TILES_OF_CHUNK, P], F32, name="bank")
-            for c in range(TILES_OF_CHUNK):
+            for b in range(TILES_OF_CHUNK // 2):
                 for i in tiles:
                     tokens = slice(i * P, (i + 1) * P)
-                    nc.tensor.matmul(
-                        out=rotated[n, i][:, c, :], lhsT=own[n][:, c, tokens], rhs=identity[:],
-                        is_transpose=True, start=True, stop=False,
-                    )
-                    nc.tensor.matmul(
-                        out=rotated[n, i][:, c, :], lhsT=partner[n][:, c, tokens], rhs=swap[:],
-                        is_transpose=True, start=False, stop=True,
-                    )
+                    for c in (2 * b, 2 * b + 1):
+                        nc.tensor.matmul(
+                            out=rotated[n, i][:, c, :], lhsT=own[n][:, c, tokens], rhs=identity[:],
+                            is_transpose=True, start=True, stop=False,
+                        )
+                        nc.tensor.matmul(
+                            out=rotated[n, i][:, c, :], lhsT=partner[n][:, c, tokens], rhs=swap[:],
+                            is_transpose=True, start=False, stop=True,
+                        )
 
         def head(n, i, h):
             return rotated[n, i][:, h // HEADS_OF_TILE, (h % HEADS_OF_TILE) * HD : (h % HEADS_OF_TILE + 1) * HD]

@@ -387,14 +387,13 @@ def tile_attention_pb_kernel(tc, x, rmskv_w, kv_w, kv_b, ln_w, out_0, out_1):
         key_root(1)
         for i in tiles:
             normalise_keys(0, i)
-        for i in tiles:
-            values(first_values, i, value_products[i])
+        last_products = [banks.tile([P, N_TILE], F32, name="bank") for i in tiles]
         for g in passes:
             quantise(last, g)
-        last_products = [banks.tile([P, N_TILE], F32, name="bank") for i in tiles]
-        for i in tiles:
-            for g in passes:
+            for i in tiles:
                 multiply_pass(last, i, g, last_products[i])
+        for i in tiles:
+            values(first_values, i, value_products[i])
         for i in tiles:
             normalise_keys(1, i)
         for i in tiles:

import concourse.mybir as mybir
from concourse.masks import make_identity

F32 = mybir.dt.float32
BF16 = mybir.dt.bfloat16
I32 = mybir.dt.int32
U32 = mybir.dt.uint32
U8 = mybir.dt.uint8
FP8X4 = mybir.dt.float8_e4m3fn_x4
ALU = mybir.AluOpType
ACT = mybir.ActivationFunctionType

B, C, D, H, ST = 32, 32, 1024, 16, 4
HD = D // H
HP = HD // 2
CS = C // ST
EPS = 1.1920929e-07

P = 128
PACK = 4
K_PASS = P * PACK
PASSES = D // K_PASS
TOKEN_TILES = B * CS // P
ROWS = P // B
N_TILE = 512
TOKENS = TOKEN_TILES * P
CHUNKS = 2 * D // N_TILE
KEY_CHUNKS = D // N_TILE
HEADS = N_TILE // HD
KEY_TILES = D // P
TILES_OF_CHUNK = N_TILE // P
HEADS_OF_TILE = P // HD

PI = 3.141592653589793
TWO_PI = 2.0 * PI
TWO_PI_HIGH = 6.28125
TWO_PI_LOW = TWO_PI - TWO_PI_HIGH
ROUND_TO_INTEGER = 1.5 * 2.0**23

FLOPS = 2 * B * CS * D * 2 * D
BYTES = 2 * (B * CS * D + D * 2 * D + D + 2 * D + HD) + 4 * 2 * B * CS * D


def rotation_phases(nc, keep, one):
    partition = keep.tile([P, 1], I32)
    nc.gpsimd.iota(partition[:], pattern=[[0, 1]], base=0, channel_multiplier=1)
    position = keep.tile([P, CS], I32)
    nc.gpsimd.iota(position[:], pattern=[[1, CS]], base=0, channel_multiplier=0)

    ratio = (1.0 + 4000.0 / 200.0) ** (1.0 / (HP - 1))
    bits = keep.tile([P, 5], I32)
    for k in range(5):
        nc.vector.tensor_single_scalar(out=bits[:, k : k + 1], in_=partition[:], scalar=2 << k, op=ALU.bitwise_and)
    odd = keep.tile([P, 1], I32)
    nc.vector.tensor_single_scalar(out=odd[:], in_=partition[:], scalar=1, op=ALU.bitwise_and)
    factors = keep.tile([P, 5], F32)
    for k in range(5):
        nc.vector.tensor_scalar(
            out=factors[:, k : k + 1], in0=bits[:, k : k + 1], scalar1=(ratio ** (1 << k) - 1.0) / (2 << k), scalar2=1.0,
            op0=ALU.mult, op1=ALU.add,
        )
    sign = keep.tile([P, 1], F32)
    nc.vector.tensor_scalar(out=sign[:], in0=odd[:], scalar1=-2.0, scalar2=1.0, op0=ALU.mult, op1=ALU.add)
    pairs = keep.tile([P, 2], F32)
    nc.vector.tensor_tensor(out=pairs[:], in0=factors[:, 0:2], in1=factors[:, 2:4], op=ALU.mult)
    power = keep.tile([P, 1], F32)
    nc.vector.scalar_tensor_tensor(
        out=power[:], in0=pairs[:, 0:1], scalar=pairs[:, 1:2], in1=factors[:, 4:5], op0=ALU.mult, op1=ALU.mult
    )
    turn = keep.tile([P, 1], F32)
    nc.vector.tensor_scalar(
        out=turn[:], in0=power[:], scalar1=1.0, scalar2=ST * 200.0 / 1000.0, op0=ALU.subtract, op1=ALU.mult
    )
    phase = keep.tile([P, 2, CS], F32)
    for a in range(2):
        nc.vector.tensor_scalar(
            out=phase[:, a, :], in0=position[:], scalar1=turn[:, 0:1], scalar2=a * 0.5 * PI, op0=ALU.mult, op1=ALU.add
        )

    turns = keep.tile([P, 2, CS], F32)
    nc.vector.tensor_scalar(
        out=turns[:], in0=phase[:], scalar1=1.0 / TWO_PI, scalar2=ROUND_TO_INTEGER, op0=ALU.mult, op1=ALU.add
    )
    nc.vector.tensor_scalar_sub(out=turns[:], in0=turns[:], scalar1=ROUND_TO_INTEGER)
    for part in (TWO_PI_HIGH, TWO_PI_LOW):
        nc.vector.scalar_tensor_tensor(
            out=phase[:], in0=turns[:], scalar=-part, in1=phase[:], op0=ALU.mult, op1=ALU.add
        )
    return phase, sign


def tile_attention_pb_kernel(tc, x, rmskv_w, kv_w, kv_b, ln_w, out_0, out_1):
    nc = tc.nc
    with (
        tc.tile_pool(name="keep", bufs=1) as keep,
        tc.tile_pool(name="stage", bufs=4) as stage,
        tc.tile_pool(name="small", bufs=4) as small,
        tc.psum_pool(name="banks", bufs=8) as banks,
        tc.manual_schedule(),
    ):
        tiles = range(TOKEN_TILES)
        passes = range(PASSES)
        first_values, last = KEY_CHUNKS, CHUNKS - 1

        x_sb = keep.tile([P, TOKEN_TILES, D], BF16)
        x_rows = x.rearrange("b t f -> (b t) f").rearrange("(p i s) f -> i s p f", i=TOKEN_TILES, s=ST)
        for i in tiles:
            nc.sync.dma_start(out=x_sb[:, i, :], in_=x_rows[i, 0])

        def load_root_table():
            nc.scalar.activation(out=warm[:], in_=one[:], func=ACT.Abs_reciprocal_sqrt)

        gain_row = keep.tile([P, D], BF16)
        nc.vector.memset(gain_row[:].bitcast(I32), 0)
        nc.sync.dma_start(out=gain_row[0:1, :], in_=rmskv_w.rearrange("(o f) -> o f", o=1))
        one = keep.tile([P, 1], F32)
        nc.vector.memset(one[:], 1.0)
        warm = keep.tile([P, 1], F32)
        load_root_table()
        vector_rows = keep.tile([P, P], BF16)
        nc.vector.memset(vector_rows[:].bitcast(I32), 0)
        nc.scalar.dma_start(out=vector_rows[0:KEY_TILES, :], in_=kv_b[0:D].rearrange("(c p) -> c p", p=P))
        ln_gain = keep.tile([P, HD], BF16)
        nc.scalar.dma_start(out=ln_gain[:], in_=ln_w.partition_broadcast(P))

        value_bias = keep.tile([P, D], BF16)
        w_rows = kv_w.rearrange("(g p t) n -> g p t n", g=PASSES, t=PACK)
        w_raw = {}
        for n in range(CHUNKS):
            for g in passes:
                w_raw[n, g] = keep.tile([P, PACK, N_TILE], BF16, name="w_raw_%d_%d" % (n, g))
                nc.sync.dma_start(out=w_raw[n, g][:], in_=w_rows[g, :, :, n * N_TILE : (n + 1) * N_TILE])
        nc.sync.dma_start(out=value_bias[:], in_=kv_b[D : 2 * D].partition_broadcast(P))

        ones = keep.tile([P, P], BF16)
        nc.vector.memset(ones[:], 1.0)
        phase, sign = rotation_phases(nc, keep, one)
        identity = keep.tile([P, P], F32)
        make_identity(nc, identity[:])
        swap = keep.tile([P, P], F32)
        for e in range(2):
            nc.vector.tensor_copy(
                out=swap[:].rearrange("p (j e) -> p e j", e=2)[:, e, :],
                in_=identity[:].rearrange("p (j e) -> p e j", e=2)[:, 1 - e, :],
            )

        w_grouped, w_codes, w_scales = {}, {}, {}

        def regroup(engine_copy, n, g):
            w_grouped[n, g] = stage.tile([P, N_TILE, PACK], BF16, name="w_grouped", align_bytes=64)
            engine_copy(
                out=w_grouped[n, g][:].rearrange("p (c i) t -> p c t i", i=4),
                in_=w_raw[n, g][:].rearrange("p t (c i) -> p c t i", i=4),
            )

        def regroup_on_gpsimd(n, g, factor=1.0):
            w_grouped[n, g] = stage.tile([P, N_TILE, PACK], BF16, name="w_grouped", align_bytes=64)
            for half in range(2):
                cols = slice(half * N_TILE // 2, (half + 1) * N_TILE // 2)
                nc.gpsimd.tensor_scalar(
                    out=w_grouped[n, g][:, cols, :], in0=w_raw[n, g][:, :, cols].rearrange("p t c -> p c t"),
                    scalar1=factor, scalar2=0.0, op0=ALU.mult, op1=ALU.add,
                )

        def gate():
            column = small.tile([P, 1], F32, name="gate")
            nc.vector.memset(column[:], 1.0)
            return column[:, 0:1]

        def quantise(n, g):
            w_codes[n, g] = keep.tile([P, N_TILE], U32, name="w_codes_%d_%d" % (n, g), align_bytes=64)
            w_scales[n, g] = keep.tile([P, N_TILE], U8, name="w_scales_%d_%d" % (n, g), align_bytes=64)
            nc.vector.quantize_mx(
                out=w_codes[n, g][:].bitcast(FP8X4), scales=w_scales[n, g][:],
                in_=w_grouped[n, g][:].rearrange("p w t -> p (w t)"),
            )

        x_sum_sq = small.tile([P, TOKEN_TILES], F32)

        def token_squares(i):
            squares = stage.tile([P, D], BF16)
            nc.scalar.activation(
                out=squares[:], in_=x_sb[:, i, :], func=ACT.Square, accum_out=x_sum_sq[:, i : i + 1]
            )

        def inverse_rms(out, sum_sq, count):
            nc.scalar.activation(out=out, in_=sum_sq, func=ACT.Abs_reciprocal_sqrt, scale=1.0 / count, bias=EPS)

        gain_all = {}
        for g in passes:
            gain_all[g] = banks.tile([P, K_PASS], F32, name="bank")
            nc.tensor.matmul(
                out=gain_all[g][:], lhsT=ones[:], rhs=gain_row[:, g * K_PASS : (g + 1) * K_PASS], start=True, stop=True
            )
        identity_bf16 = keep.tile([P, P], BF16)
        nc.vector.tensor_copy(out=identity_bf16[:], in_=identity[:])

        x_normed, x_turned, x_grouped, x_codes, x_scales = {}, {}, {}, {}, {}

        def norm_tokens(i, g):
            x_normed[i, g] = stage.tile([P, K_PASS], BF16, name="x_normed")
            nc.vector.scalar_tensor_tensor(
                out=x_normed[i, g][:], in0=x_sb[:, i, g * K_PASS : (g + 1) * K_PASS], scalar=x_inverse[:, i : i + 1],
                in1=gain_all[g][:], op0=ALU.mult, op1=ALU.mult,
            )

        def turn_tokens(g):
            x_turned[g] = banks.tile([P, TOKEN_TILES, 2, P], F32, name="bank")
            for i in tiles:
                for u in range(2):
                    nc.tensor.transpose(x_turned[g][:, i, u, :], x_normed[i, g][:].bitcast(F32)[:, u::2], identity[:])

        def gather_tokens(g):
            x_grouped[g] = stage.tile([P, TOKEN_TILES, P, PACK], BF16, name="x_grouped", align_bytes=64)
            nc.scalar.copy(out=x_grouped[g][:].bitcast(F32), in_=x_turned[g][:].rearrange("p i u r -> p i r u"))

        def quantise_tokens(g):
            x_codes[g] = keep.tile([P, TOKENS], U32, name="x_codes_%d" % g, align_bytes=64)
            x_scales[g] = keep.tile([P, TOKENS], U8, name="x_scales_%d" % g, align_bytes=64)
            nc.vector.quantize_mx(
                out=x_codes[g][:].bitcast(FP8X4), scales=x_scales[g][:],
                in_=x_grouped[g][:].rearrange("p i r t -> p (i r t)"),
            )

        key_products, key_sums, key_inverse, own, partner, rotated = {}, {}, {}, {}, {}, {}

        def multiply_keys(n):
            for b in range(TILES_OF_CHUNK // 2):
                key_products[n, b] = banks.tile([P, 2, TOKENS], F32, name="bank")
                for k in range(2):
                    channels = slice((2 * b + k) * P, (2 * b + k + 1) * P)
                    for g in passes:
                        nc.tensor.matmul_mx(
                            out=key_products[n, b][:, k, :],
                            lhsT=w_codes[n, g][:, channels].bitcast(FP8X4), lhsT_scale=w_scales[n, g][:, channels],
                            rhs=x_codes[g][:].bitcast(FP8X4), rhs_scale=x_scales[g][:],
                            start=(g == 0), stop=(g == PASSES - 1),
                        )

        def weigh_keys(n, b):
            for k in range(2):
                c = 2 * b + k
                for weighed, factor in ((own, own_factor), (partner, partner_factor)):
                    nc.vector.scalar_tensor_tensor(
                        out=weighed[n][:, c, :], in0=key_products[n, b][:, k, :],
                        scalar=key_bias[:, n * TILES_OF_CHUNK + c : n * TILES_OF_CHUNK + c + 1],
                        in1=factor[:], op0=ALU.add, op1=ALU.mult,
                    )

        def weigh_chunk(n):
            own[n] = stage.tile([P, TILES_OF_CHUNK, TOKENS], F32, name="own")
            partner[n] = stage.tile([P, TILES_OF_CHUNK, TOKENS], F32, name="partner")
            for b in range(TILES_OF_CHUNK // 2):
                weigh_keys(n, b)

        def turn_keys(n):
            for i in tiles:
                rotated[n, i] = banks.tile([P, TILES_OF_CHUNK, P], F32, name="bank")
            for b in range(TILES_OF_CHUNK // 2):
                for i in tiles:
                    tokens = slice(i * P, (i + 1) * P)
                    for c in (2 * b, 2 * b + 1):
                        nc.tensor.matmul(
                            out=rotated[n, i][:, c, :], lhsT=own[n][:, c, tokens], rhs=identity[:],
                            is_transpose=True, start=True, stop=False,
                        )
                        nc.tensor.matmul(
                            out=rotated[n, i][:, c, :], lhsT=partner[n][:, c, tokens], rhs=swap[:],
                            is_transpose=True, start=False, stop=True,
                        )

        def head(n, i, h):
            return rotated[n, i][:, h // HEADS_OF_TILE, (h % HEADS_OF_TILE) * HD : (h % HEADS_OF_TILE + 1) * HD]

        def sum_squares(n):
            squares = stage.tile([P, HEADS, HD], F32, name="head_squares")
            key_sums[n] = small.tile([P, TOKEN_TILES, HEADS], F32, name="key_sums")
            for i in tiles:
                for h in range(HEADS):
                    nc.scalar.activation(
                        out=squares[:, h, :], in_=head(n, i, h), func=ACT.Square, accum_out=key_sums[n][:, i, h : h + 1]
                    )

        def key_root(n):
            key_inverse[n] = small.tile([P, TOKEN_TILES, HEADS], F32, name="key_inverse")
            inverse_rms(key_inverse[n][:], key_sums[n][:], HD)

        results = {}

        def store(out, first_head, result):
            for r in range(ROWS):
                nc.sync.dma_start(
                    out=out[:, first_head : first_head + HEADS, TOKEN_TILES * r : TOKEN_TILES * (r + 1), :].rearrange(
                        "b h i d -> b h (i d)"
                    ),
                    in_=result[r:P:ROWS, :, :, :].rearrange("p h i d -> p h (i d)"),
                )

        def normalise_keys(n, i):
            if i == 0:
                results[n] = stage.tile([P, HEADS, TOKEN_TILES, HD], F32, name="key_result")
            for h in range(HEADS):
                nc.vector.scalar_tensor_tensor(
                    out=results[n][:, h, i, :], in0=head(n, i, h), scalar=key_inverse[n][:, i, h : h + 1], in1=ln_gain[:],
                    op0=ALU.mult, op1=ALU.mult,
                )
            if i == TOKEN_TILES - 1:
                store(out_0, n * HEADS, results[n])

        def multiply_pass(n, i, g, product):
            tokens = slice(i * P, (i + 1) * P)
            nc.tensor.matmul_mx(
                out=product[:],
                lhsT=x_codes[g][:, tokens].bitcast(FP8X4), lhsT_scale=x_scales[g][:, tokens],
                rhs=w_codes[n, g][:].bitcast(FP8X4), rhs_scale=w_scales[n, g][:],
                start=(g == 0), stop=(g == PASSES - 1),
            )

        def values(n, i, product):
            if i == 0:
                results[n] = stage.tile([P, HEADS, TOKEN_TILES, HD], F32, name="value_result")
            columns_of_chunk = slice((n - KEY_CHUNKS) * N_TILE, (n - KEY_CHUNKS + 1) * N_TILE)
            nc.vector.tensor_tensor(
                out=results[n][:, :, i, :], in0=product[:].rearrange("p (h d) -> p h d", d=HD),
                in1=value_bias[:, columns_of_chunk].rearrange("p (h d) -> p h d", d=HD), op=ALU.add,
            )
            if i == TOKEN_TILES - 1:
                store(out_1, (n - KEY_CHUNKS) * HEADS, results[n])

        for i in tiles:
            token_squares(i)
        x_inverse = small.tile([P, TOKEN_TILES], F32)
        inverse_rms(x_inverse[:], x_sum_sq[:], D)
        regroup(nc.vector.tensor_copy, 0, 0)
        for g in passes:
            for i in tiles:
                norm_tokens(i, g)
            turn_tokens(g)
        sin_cos = keep.tile([P, 2, CS], F32)
        nc.scalar.activation(out=sin_cos[:], in_=phase[:], func=ACT.Sin)
        for g in passes:
            gather_tokens(g)
        load_root_table()
        vector_columns = banks.tile([P, P], BF16, name="bank")
        nc.tensor.transpose(vector_columns[:], vector_rows[:], identity_bf16[:])
        regroup_on_gpsimd(0, 1)
        quantise(0, 0)
        quantise_tokens(0)
        quantise(0, 1)
        quantise_tokens(1)
        key_bias = keep.tile([P, KEY_TILES], F32)
        nc.vector.tensor_copy(out=key_bias[:], in_=vector_columns[:, 0:KEY_TILES])
        multiply_keys(0)
        regroup(nc.scalar.copy, 1, 1)
        regroup(nc.vector.tensor_copy, 1, 0)
        own_factor = keep.tile([P, TOKENS], F32)
        partner_factor = keep.tile([P, TOKENS], F32)
        for factor, table, by in ((own_factor, 1, 1.0), (partner_factor, 0, sign[:, 0:1])):
            nc.vector.tensor_scalar_mul(
                out=factor[:].rearrange("p (i b r) -> p i b r", i=TOKEN_TILES, r=ROWS),
                in0=sin_cos[:, table, :].rearrange("p (r i) -> p i r", r=ROWS).unsqueeze(2).to_broadcast(
                    [P, TOKEN_TILES, B, ROWS]
                ),
                scalar1=by,
            )

        regroup_on_gpsimd(first_values, 1, gate())
        weigh_chunk(0)
        turn_keys(0)
        regroup(nc.scalar.copy, first_values, 0)
        sum_squares(0)
        key_root(0)
        for g in passes:
            quantise(1, g)
        multiply_keys(1)
        for g in passes:
            quantise(first_values, g)
        value_products = [banks.tile([P, N_TILE], F32, name="bank") for i in tiles]
        for i in tiles:
            for g in passes:
                multiply_pass(first_values, i, g, value_products[i])
        regroup(nc.scalar.copy, last, 1)
        regroup_on_gpsimd(last, 0, gate())
        weigh_chunk(1)
        turn_keys(1)
        sum_squares(1)
        key_root(1)
        for i in tiles:
            normalise_keys(0, i)
        last_products = [banks.tile([P, N_TILE], F32, name="bank") for i in tiles]
        for g in passes:
            quantise(last, g)
            for i in tiles:
                multiply_pass(last, i, g, last_products[i])
        for i in tiles:
            values(first_values, i, value_products[i])
        for i in tiles:
            normalise_keys(1, i)
        for i in tiles:
            values(last, i, last_products[i])
